import numpy as np
import ml_dtypes


def mxq(x, axis, fmt="e4m3"):
    dtype, down = {"e4m3": (ml_dtypes.float8_e4m3fn, 7), "e5m2": (ml_dtypes.float8_e5m2, 14)}[fmt]
    v = np.moveaxis(np.asarray(x, np.float32).astype(ml_dtypes.bfloat16).astype(np.float64), axis, -1)
    blocks = v.reshape(v.shape[:-1] + (-1, 32))
    amax = np.abs(blocks).max(-1, keepdims=True)
    byte = np.maximum(np.where(amax > 0, np.frexp(amax)[1] - 1 + 127, 0) - down, 1)
    scale = np.exp2(byte - 127.0)
    codes = (blocks / scale).astype(np.float32).astype(dtype).astype(np.float64)
    return np.moveaxis((codes * scale).reshape(v.shape), -1, axis)


WIDE = False


def mx_kscale(k):
    if not WIDE:
        return np.ones(k)
    levels = np.array([10, -10, 5, -5, 0])
    a = np.random.permutation(np.resize(levels, k // 512 * 4)).reshape(k // 512, 4)
    idx = np.arange(k)
    return np.exp2(a[idx // 512, idx % 128 // 32])


BF16 = ml_dtypes.bfloat16


def bf(x):
    return np.asarray(x, np.float32).astype(BF16)


def f64(x):
    return np.asarray(x).astype(np.float64)


B, N, C, H, F = 2, 512, 1024, 8, 2752
D = C // H


def setup_inputs():
    a = mx_kscale(C)[:D]
    t = np.tile(a, H)
    z = np.random.standard_normal((B, H, D, D)) * np.sqrt((N + N * N / C) / D)
    e = np.exp(z - z.max(-1, keepdims=True))
    return {"attn": bf(e / e.sum(-1, keepdims=True) * a[:, None]),
            "v": bf(np.random.standard_normal((B, H, N, D))),
            "w_proj": bf(np.random.standard_normal((C, C)) / np.sqrt(C) / t),
            "b_proj": bf(0.1 * np.random.standard_normal(C)),
            "shortcut": bf(np.random.standard_normal((B, N, C)))}


def reference(attn, v, w_proj, b_proj, shortcut):
    o = f64(attn) @ f64(v).transpose(0, 1, 3, 2)
    o = o.transpose(0, 1, 3, 2).reshape(B, N, C)
    return (mxq(o, 2, "e4m3") @ mxq(f64(w_proj), 1, "e4m3").T) + f64(b_proj) + f64(shortcut)

@@ -1,0 +1,194 @@
+from contextlib import ExitStack
+
+import concourse.mybir as mybir
+from concourse.masks import make_identity
+
+BF16 = mybir.dt.bfloat16
+F32 = mybir.dt.float32
+U32 = mybir.dt.uint32
+U8 = mybir.dt.uint8
+FP8X4 = mybir.dt.float8_e4m3fn_x4
+ADD = mybir.AluOpType.add
+
+P = 128
+BATCH, HEADS, TOKENS, C = 2, 8, 512, 1024
+CHUNKS = C // P
+PACK = 4
+PASSES = C // (P * PACK)
+ROW_TILES = BATCH * TOKENS // P
+HEAD_ROWS = TOKENS // CHUNKS
+GROUPS = ROW_TILES // 2
+BANK = 512
+HALVES = C // BANK
+
+FLOPS = 2 * BATCH * HEADS * P * P * TOKENS + 2 * BATCH * TOKENS * C * C
+
+
+def tile_transposedattentiontransformer_pb_kernel(tc, attn, v, w_proj, b_proj, shortcut, out):
+    nc = tc.nc
+    v_rows = v.flatten_outer_dims().rearrange("(r s) e -> r (s e)", s=CHUNKS)
+    shortcut_rows = shortcut.flatten_outer_dims()
+    out_rows = out.flatten_outer_dims()
+
+    with ExitStack() as ctx:
+        keep = ctx.enter_context(tc.tile_pool(name="keep", bufs=1))
+        work = ctx.enter_context(tc.tile_pool(name="work", bufs=3))
+        psum = ctx.enter_context(tc.psum_pool(name="psum", bufs=1))
+
+        def load_two_row_tiles(rows, group, name):
+            pair = keep.tile([P, 2, C], BF16, name=name)
+            nc.sync.dma_start(
+                out=pair[:],
+                in_=rows[2 * P * group : 2 * P * (group + 1), :].rearrange("(i p) c -> p i c", p=P),
+            )
+            return pair
+
+        def load_attn(b):
+            heads = keep.tile([P, HEADS, P], BF16, name="attn_sb%d" % b)
+            nc.sync.dma_start(out=heads[:], in_=attn[b].rearrange("g d e -> d g e"))
+            return heads
+
+        ident = keep.tile([P, P], BF16, name="ident")
+        make_identity(nc, ident[:])
+        ones = keep.tile([P, P], BF16, name="ones")
+        nc.vector.memset(ones[:], 1.0)
+        bias_rows = keep.tile([P, C], BF16, name="bias_rows")
+        nc.vector.memset(bias_rows[:], 0.0)
+
+        attn_sb = [load_attn(0)]
+        v_sb = [load_two_row_tiles(v_rows, 0, "v_sb0")]
+        nc.sync.dma_start(out=bias_rows[0:1, :], in_=b_proj.rearrange("(o c) -> o c", o=1))
+        v_sb.append(load_two_row_tiles(v_rows, 1, "v_sb1"))
+        shortcut_sb = [load_two_row_tiles(shortcut_rows, 0, "shortcut_sb0")]
+        w_sb = [load_two_row_tiles(w_proj, k, "w_sb%d" % k) for k in range(GROUPS)]
+        shortcut_sb.append(load_two_row_tiles(shortcut_rows, 1, "shortcut_sb1"))
+        attn_sb.append(load_attn(1))
+        for group in range(2, GROUPS):
+            v_sb.append(load_two_row_tiles(v_rows, group, "v_sb%d" % group))
+            shortcut_sb.append(load_two_row_tiles(shortcut_rows, group, "shortcut_sb%d" % group))
+
+        attn_T = []
+
+        def transpose_attn(b):
+            flipped = psum.tile([P, HEADS, P], BF16, tag="flip", bufs=3)
+            for g in range(HEADS):
+                nc.tensor.transpose(flipped[:, g, :], attn_sb[b][:, g, :], ident[:])
+            heads_T = keep.tile([P, HEADS, P], BF16, name="attn_T%d" % b)
+            nc.scalar.copy(out=heads_T[:], in_=flipped[:])
+            attn_T.append(heads_T)
+
+        y_codes = []
+        y_scales = []
+
+        def first_stage(tile_i):
+            rows = v_sb[tile_i // 2][:, tile_i % 2, :]
+            flipped = psum.tile([P, CHUNKS, P], BF16, tag="flip", bufs=3)
+            for s in range(CHUNKS):
+                nc.tensor.transpose(flipped[:, s, :], rows[:, s * P : (s + 1) * P], ident[:])
+            v_T = work.tile([P, CHUNKS, P], BF16)
+            nc.scalar.copy(out=v_T[:], in_=flipped[:])
+
+            grouped = work.tile([P, PASSES, P, PACK], BF16, align_bytes=64)
+            for h in range(2):
+                head = 2 * tile_i + h
+                head_rows = slice(h * HEAD_ROWS, (h + 1) * HEAD_ROWS)
+                o = psum.tile([P, CHUNKS, HEAD_ROWS], F32, tag="o", bufs=2)
+                nc.tensor.matmul(
+                    o[:], lhsT=attn_T[head // HEADS][:, head % HEADS, :], rhs=v_T[:, :, head_rows], start=True, stop=True
+                )
+                if h == 1 and tile_i < 4:
+                    nc.vector.tensor_copy(
+                        out=grouped[:, :, head_rows, :], in_=o[:].rearrange("p (c t) r -> p c r t", t=PACK)
+                    )
+                else:
+                    nc.scalar.copy(
+                        out=grouped[:, :, head_rows, :], in_=o[:].rearrange("p (c t) r -> p c r t", t=PACK)
+                    )
+            codes = keep.tile([P, PASSES, P], U32, name="y_codes%d" % tile_i, align_bytes=64)
+            scales = keep.tile([P, PASSES, P], U8, name="y_scales%d" % tile_i, align_bytes=64)
+            nc.vector.quantize_mx(
+                out=codes[:].rearrange("p c r -> p (c r)").bitcast(FP8X4),
+                scales=scales[:].rearrange("p c r -> p (c r)"),
+                in_=grouped[:].rearrange("p c r t -> p (c r t)"),
+            )
+            y_codes.append(codes)
+            y_scales.append(scales)
+
+        w_grouped = keep.tile([P, PASSES, C, PACK], BF16, name="w_grouped", align_bytes=64)
+        w_codes = keep.tile([P, PASSES, C], U32, name="w_codes", align_bytes=64)
+        w_scales = keep.tile([P, PASSES, C], U8, name="w_scales", align_bytes=64)
+
+        def transpose_w(j_tile):
+            rows = w_sb[j_tile // 2][:, j_tile % 2, :]
+            flipped = psum.tile([P, PASSES, PACK, P], BF16, tag="flip", bufs=3)
+            for c in range(PASSES):
+                for t in range(PACK):
+                    k0 = (c * PACK + t) * P
+                    nc.tensor.transpose(flipped[:, c, t, :], rows[:, k0 : k0 + P], ident[:])
+            dst = w_grouped[:, :, j_tile * P : (j_tile + 1) * P, :]
+            src = flipped[:].rearrange("p c t j -> p c j t")
+            if j_tile % 2 == 0:
+                nc.scalar.copy(out=dst, in_=src)
+            else:
+                nc.vector.tensor_copy(out=dst, in_=src)
+
+        def quantise_w(half):
+            cols = slice(half * BANK, (half + 1) * BANK)
+            for c in range(PASSES):
+                nc.vector.quantize_mx(
+                    out=w_codes[:, c, cols].bitcast(FP8X4),
+                    scales=w_scales[:, c, cols],
+                    in_=w_grouped[:, c, cols, :].rearrange("p j t -> p (j t)"),
+                )
+
+        def second_stage(tile_i):
+            for half in range(HALVES):
+                cols = slice(half * BANK, (half + 1) * BANK)
+                acc = psum.tile([P, BANK], F32, tag="acc", bufs=3)
+                for c in range(PASSES):
+                    nc.tensor.matmul_mx(
+                        out=acc[:],
+                        lhsT=y_codes[tile_i][:, c, :].bitcast(FP8X4),
+                        lhsT_scale=y_scales[tile_i][:, c, :],
+                        rhs=w_codes[:, c, cols].bitcast(FP8X4),
+                        rhs_scale=w_scales[:, c, cols],
+                        start=(c == 0),
+                        stop=(c == PASSES - 1),
+                    )
+                nc.vector.tensor_tensor(out=residual[tile_i][:, cols], in0=acc[:], in1=residual[tile_i][:, cols], op=ADD)
+            nc.sync.dma_start(out=out_rows[tile_i * P : (tile_i + 1) * P, :], in_=residual[tile_i][:])
+
+        def first_stage_of_group(group):
+            if group % 2 == 0:
+                transpose_attn(group // 2)
+            first_stage(2 * group)
+            first_stage(2 * group + 1)
+
+        first_stage_of_group(0)
+        bias_all = keep.tile([P, C], BF16, name="bias_all")
+        for half in range(HALVES):
+            cols = slice(half * BANK, (half + 1) * BANK)
+            spread = psum.tile([P, BANK], F32, tag="acc", bufs=3)
+            nc.tensor.matmul(spread[:], lhsT=ones[:], rhs=bias_rows[:, cols], start=True, stop=True)
+            nc.scalar.copy(out=bias_all[:, cols], in_=spread[:])
+
+        residual = []
+        for tile_i in range(ROW_TILES):
+            summed = keep.tile([P, C], F32, name="residual%d" % tile_i)
+            for half in range(HALVES):
+                cols = slice(half * BANK, (half + 1) * BANK)
+                nc.gpsimd.tensor_tensor(
+                    out=summed[:, cols], in0=shortcut_sb[tile_i // 2][:, tile_i % 2, cols], in1=bias_all[:, cols], op=ADD
+                )
+            residual.append(summed)
+
+        first_stage_of_group(1)
+        for j_tile in range(ROW_TILES):
+            transpose_w(j_tile)
+            if j_tile % 4 == 3:
+                quantise_w(j_tile // 4)
+        for group in range(GROUPS):
+            second_stage(2 * group)
+            second_stage(2 * group + 1)
+            if group + 2 < GROUPS:
+                first_stage_of_group(group + 2)

@@ -18,6 +18,9 @@ PASSES = C // (P * PACK)
 ROW_TILES = BATCH * TOKENS // P
 HEAD_ROWS = TOKENS // CHUNKS
 GROUPS = ROW_TILES // 2
+SIDES = 2
+HALF_ROW = C // SIDES
+PAIRS = PACK // SIDES
 BANK = 512
 HALVES = C // BANK
 
@@ -26,7 +29,8 @@ FLOPS = 2 * BATCH * HEADS * P * P * TOKENS + 2 * BATCH * TOKENS * C * C
 
 def tile_transposedattentiontransformer_pb_kernel(tc, attn, v, w_proj, b_proj, shortcut, out):
     nc = tc.nc
-    v_rows = v.flatten_outer_dims().rearrange("(r s) e -> r (s e)", s=CHUNKS)
+    v_halves = v.flatten_outer_dims().rearrange("(q s) e -> q (s e)", s=CHUNKS // SIDES)
+    w_halves = w_proj.rearrange("j (u k) -> (j u) k", u=SIDES)
     shortcut_rows = shortcut.flatten_outer_dims()
     out_rows = out.flatten_outer_dims()
 
@@ -43,6 +47,14 @@ def tile_transposedattentiontransformer_pb_kernel(tc, attn, v, w_proj, b_proj, s
             )
             return pair
 
+        def load_four_blocks(halves, group, name):
+            four = keep.tile([P, 2 * SIDES, HALF_ROW], BF16, name=name)
+            nc.sync.dma_start(
+                out=four[:],
+                in_=halves[4 * P * group : 4 * P * (group + 1), :].rearrange("(i p) x -> p i x", p=P),
+            )
+            return four
+
         def load_attn(b):
             heads = keep.tile([P, HEADS, P], BF16, name="attn_sb%d" % b)
             nc.sync.dma_start(out=heads[:], in_=attn[b].rearrange("g d e -> d g e"))
@@ -56,16 +68,19 @@ def tile_transposedattentiontransformer_pb_kernel(tc, attn, v, w_proj, b_proj, s
         nc.vector.memset(bias_rows[:], 0.0)
 
         attn_sb = [load_attn(0)]
-        v_sb = [load_two_row_tiles(v_rows, 0, "v_sb0")]
+        v_sb = [load_four_blocks(v_halves, 0, "v_sb0")]
         nc.sync.dma_start(out=bias_rows[0:1, :], in_=b_proj.rearrange("(o c) -> o c", o=1))
-        v_sb.append(load_two_row_tiles(v_rows, 1, "v_sb1"))
+        v_sb.append(load_four_blocks(v_halves, 1, "v_sb1"))
         shortcut_sb = [load_two_row_tiles(shortcut_rows, 0, "shortcut_sb0")]
-        w_sb = [load_two_row_tiles(w_proj, k, "w_sb%d" % k) for k in range(GROUPS)]
+        w_sb = [load_four_blocks(w_halves, k, "w_sb%d" % k) for k in range(GROUPS)]
         shortcut_sb.append(load_two_row_tiles(shortcut_rows, 1, "shortcut_sb1"))
         attn_sb.append(load_attn(1))
         for group in range(2, GROUPS):
-            v_sb.append(load_two_row_tiles(v_rows, group, "v_sb%d" % group))
+            v_sb.append(load_four_blocks(v_halves, group, "v_sb%d" % group))
             shortcut_sb.append(load_two_row_tiles(shortcut_rows, group, "shortcut_sb%d" % group))
+
+        def words(ap, merge):
+            return ap.rearrange(merge).bitcast(F32)
 
         attn_T = []
 
@@ -74,36 +89,38 @@ def tile_transposedattentiontransformer_pb_kernel(tc, attn, v, w_proj, b_proj, s
             for g in range(HEADS):
                 nc.tensor.transpose(flipped[:, g, :], attn_sb[b][:, g, :], ident[:])
             heads_T = keep.tile([P, HEADS, P], BF16, name="attn_T%d" % b)
-            nc.scalar.copy(out=heads_T[:], in_=flipped[:])
+            nc.scalar.copy(out=words(heads_T[:], "p g d -> p (g d)"), in_=words(flipped[:], "p g d -> p (g d)"))
             attn_T.append(heads_T)
 
         y_codes = []
         y_scales = []
 
         def first_stage(tile_i):
-            rows = v_sb[tile_i // 2][:, tile_i % 2, :]
-            flipped = psum.tile([P, CHUNKS, P], BF16, tag="flip", bufs=3)
-            for s in range(CHUNKS):
-                nc.tensor.transpose(flipped[:, s, :], rows[:, s * P : (s + 1) * P], ident[:])
-            v_T = work.tile([P, CHUNKS, P], BF16)
-            nc.scalar.copy(out=v_T[:], in_=flipped[:])
+            flipped = psum.tile([P, 2, CHUNKS // SIDES, P], BF16, tag="flip", bufs=3)
+            for h in range(2):
+                block = v_sb[tile_i // 2][:, 2 * (tile_i % 2) + h, :]
+                for s in range(CHUNKS // SIDES):
+                    nc.tensor.transpose(flipped[:, h, s, :], block[:, s * P : (s + 1) * P], ident[:])
+            v_T = work.tile([P, 2, CHUNKS // SIDES, P], BF16)
+            nc.scalar.copy(out=words(v_T[:], "p h s q -> p (h s q)"), in_=words(flipped[:], "p h s q -> p (h s q)"))
 
-            grouped = work.tile([P, PASSES, P, PACK], BF16, align_bytes=64)
+            o = psum.tile([P, PASSES, 2, HEAD_ROWS, PAIRS, SIDES], BF16, tag="o", bufs=2)
             for h in range(2):
                 head = 2 * tile_i + h
-                head_rows = slice(h * HEAD_ROWS, (h + 1) * HEAD_ROWS)
-                o = psum.tile([P, CHUNKS, HEAD_ROWS], F32, tag="o", bufs=2)
-                nc.tensor.matmul(
-                    o[:], lhsT=attn_T[head // HEADS][:, head % HEADS, :], rhs=v_T[:, :, head_rows], start=True, stop=True
-                )
-                if h == 1 and tile_i < 4:
-                    nc.vector.tensor_copy(
-                        out=grouped[:, :, head_rows, :], in_=o[:].rearrange("p (c t) r -> p c r t", t=PACK)
+                for c in range(PASSES):
+                    nc.tensor.matmul(
+                        o[:, c, h].rearrange("p r s u -> p s r u"),
+                        lhsT=attn_T[head // HEADS][:, head % HEADS, :],
+                        rhs=v_T[:, h, PAIRS * c : PAIRS * (c + 1), :].rearrange("p s (r u) -> p s r u", u=SIDES),
+                        start=True,
+                        stop=True,
                     )
-                else:
-                    nc.scalar.copy(
-                        out=grouped[:, :, head_rows, :], in_=o[:].rearrange("p (c t) r -> p c r t", t=PACK)
-                    )
+            grouped = work.tile([P, PASSES, P, PACK], BF16, align_bytes=64)
+            moved = grouped[:].rearrange("p c r t -> p (c r t)")
+            if tile_i < 4:
+                nc.vector.tensor_copy(out=moved, in_=o[:].rearrange("p c h r s u -> p (c h r s u)"))
+            else:
+                nc.scalar.copy(out=moved, in_=o[:].rearrange("p c h r s u -> p (c h r s u)"))
             codes = keep.tile([P, PASSES, P], U32, name="y_codes%d" % tile_i, align_bytes=64)
             scales = keep.tile([P, PASSES, P], U8, name="y_scales%d" % tile_i, align_bytes=64)
             nc.vector.quantize_mx(
@@ -119,18 +136,21 @@ def tile_transposedattentiontransformer_pb_kernel(tc, attn, v, w_proj, b_proj, s
         w_scales = keep.tile([P, PASSES, C], U8, name="w_scales", align_bytes=64)
 
         def transpose_w(j_tile):
-            rows = w_sb[j_tile // 2][:, j_tile % 2, :]
-            flipped = psum.tile([P, PASSES, PACK, P], BF16, tag="flip", bufs=3)
-            for c in range(PASSES):
-                for t in range(PACK):
-                    k0 = (c * PACK + t) * P
-                    nc.tensor.transpose(flipped[:, c, t, :], rows[:, k0 : k0 + P], ident[:])
-            dst = w_grouped[:, :, j_tile * P : (j_tile + 1) * P, :]
-            src = flipped[:].rearrange("p c t j -> p c j t")
+            flipped = psum.tile([P, PASSES, P, PAIRS, SIDES], BF16, tag="flip", bufs=3)
+            for i in range(2):
+                block = w_sb[j_tile // 2][:, 2 * (j_tile % 2) + i, :]
+                for c in range(PASSES):
+                    for s in range(PAIRS):
+                        k0 = (c * PAIRS + s) * P
+                        nc.tensor.transpose(
+                            flipped[:, c, i * HEAD_ROWS : (i + 1) * HEAD_ROWS, s, :], block[:, k0 : k0 + P], ident[:]
+                        )
+            dst = w_grouped[:, :, j_tile * P : (j_tile + 1) * P, :].rearrange("p c j t -> p c (j t)").bitcast(F32)
+            moved = flipped[:].rearrange("p c j s u -> p c (j s u)").bitcast(F32)
             if j_tile % 2 == 0:
-                nc.scalar.copy(out=dst, in_=src)
+                nc.scalar.copy(out=dst, in_=moved)
             else:
-                nc.vector.tensor_copy(out=dst, in_=src)
+                nc.vector.tensor_copy(out=dst, in_=moved)
 
         def quantise_w(half):
             cols = slice(half * BANK, (half + 1) * BANK)

@@ -18,18 +18,19 @@ PASSES = C // (P * PACK)
 ROW_TILES = BATCH * TOKENS // P
 HEAD_ROWS = TOKENS // CHUNKS
 GROUPS = ROW_TILES // 2
-SIDES = 2
-HALF_ROW = C // SIDES
-PAIRS = PACK // SIDES
 BANK = 512
 HALVES = C // BANK
+SIDES = 2
+HALF_ROW = C // SIDES
+SIDE_CHUNKS = CHUNKS // SIDES
+PAIRS = PACK // SIDES
 
 FLOPS = 2 * BATCH * HEADS * P * P * TOKENS + 2 * BATCH * TOKENS * C * C
 
 
 def tile_transposedattentiontransformer_pb_kernel(tc, attn, v, w_proj, b_proj, shortcut, out):
     nc = tc.nc
-    v_halves = v.flatten_outer_dims().rearrange("(q s) e -> q (s e)", s=CHUNKS // SIDES)
+    v_halves = v.flatten_outer_dims().rearrange("(q s) e -> q (s e)", s=SIDE_CHUNKS)
     w_halves = w_proj.rearrange("j (u k) -> (j u) k", u=SIDES)
     shortcut_rows = shortcut.flatten_outer_dims()
     out_rows = out.flatten_outer_dims()
@@ -39,14 +40,6 @@ def tile_transposedattentiontransformer_pb_kernel(tc, attn, v, w_proj, b_proj, s
         work = ctx.enter_context(tc.tile_pool(name="work", bufs=3))
         psum = ctx.enter_context(tc.psum_pool(name="psum", bufs=1))
 
-        def load_two_row_tiles(rows, group, name):
-            pair = keep.tile([P, 2, C], BF16, name=name)
-            nc.sync.dma_start(
-                out=pair[:],
-                in_=rows[2 * P * group : 2 * P * (group + 1), :].rearrange("(i p) c -> p i c", p=P),
-            )
-            return pair
-
         def load_four_blocks(halves, group, name):
             four = keep.tile([P, 2 * SIDES, HALF_ROW], BF16, name=name)
             nc.sync.dma_start(
@@ -55,10 +48,21 @@ def tile_transposedattentiontransformer_pb_kernel(tc, attn, v, w_proj, b_proj, s
             )
             return four
 
+        def load_shortcut(group):
+            pair = keep.tile([P, 2, C], BF16, name="shortcut_sb%d" % group)
+            nc.sync.dma_start(
+                out=pair[:],
+                in_=shortcut_rows[2 * P * group : 2 * P * (group + 1), :].rearrange("(i p) c -> p i c", p=P),
+            )
+            return pair
+
         def load_attn(b):
             heads = keep.tile([P, HEADS, P], BF16, name="attn_sb%d" % b)
             nc.sync.dma_start(out=heads[:], in_=attn[b].rearrange("g d e -> d g e"))
             return heads
+
+        def words(ap, merge):
+            return ap.rearrange(merge).bitcast(F32)
 
         ident = keep.tile([P, P], BF16, name="ident")
         make_identity(nc, ident[:])
@@ -67,76 +71,73 @@ def tile_transposedattentiontransformer_pb_kernel(tc, attn, v, w_proj, b_proj, s
         bias_rows = keep.tile([P, C], BF16, name="bias_rows")
         nc.vector.memset(bias_rows[:], 0.0)
 
-        attn_sb = [load_attn(0)]
-        v_sb = [load_four_blocks(v_halves, 0, "v_sb0")]
-        nc.sync.dma_start(out=bias_rows[0:1, :], in_=b_proj.rearrange("(o c) -> o c", o=1))
-        v_sb.append(load_four_blocks(v_halves, 1, "v_sb1"))
-        shortcut_sb = [load_two_row_tiles(shortcut_rows, 0, "shortcut_sb0")]
-        w_sb = [load_four_blocks(w_halves, k, "w_sb%d" % k) for k in range(GROUPS)]
-        shortcut_sb.append(load_two_row_tiles(shortcut_rows, 1, "shortcut_sb1"))
-        attn_sb.append(load_attn(1))
-        for group in range(2, GROUPS):
-            v_sb.append(load_four_blocks(v_halves, group, "v_sb%d" % group))
-            shortcut_sb.append(load_two_row_tiles(shortcut_rows, group, "shortcut_sb%d" % group))
-
-        def words(ap, merge):
-            return ap.rearrange(merge).bitcast(F32)
-
-        attn_T = []
-
-        def transpose_attn(b):
-            flipped = psum.tile([P, HEADS, P], BF16, tag="flip", bufs=3)
-            for g in range(HEADS):
-                nc.tensor.transpose(flipped[:, g, :], attn_sb[b][:, g, :], ident[:])
-            heads_T = keep.tile([P, HEADS, P], BF16, name="attn_T%d" % b)
-            nc.scalar.copy(out=words(heads_T[:], "p g d -> p (g d)"), in_=words(flipped[:], "p g d -> p (g d)"))
-            attn_T.append(heads_T)
-
-        y_codes = []
-        y_scales = []
-
-        def first_stage(tile_i):
-            flipped = psum.tile([P, 2, CHUNKS // SIDES, P], BF16, tag="flip", bufs=3)
-            for h in range(2):
-                block = v_sb[tile_i // 2][:, 2 * (tile_i % 2) + h, :]
-                for s in range(CHUNKS // SIDES):
-                    nc.tensor.transpose(flipped[:, h, s, :], block[:, s * P : (s + 1) * P], ident[:])
-            v_T = work.tile([P, 2, CHUNKS // SIDES, P], BF16)
-            nc.scalar.copy(out=words(v_T[:], "p h s q -> p (h s q)"), in_=words(flipped[:], "p h s q -> p (h s q)"))
-
-            o = psum.tile([P, PASSES, 2, HEAD_ROWS, PAIRS, SIDES], BF16, tag="o", bufs=2)
-            for h in range(2):
-                head = 2 * tile_i + h
-                for c in range(PASSES):
-                    nc.tensor.matmul(
-                        o[:, c, h].rearrange("p r s u -> p s r u"),
-                        lhsT=attn_T[head // HEADS][:, head % HEADS, :],
-                        rhs=v_T[:, h, PAIRS * c : PAIRS * (c + 1), :].rearrange("p s (r u) -> p s r u", u=SIDES),
-                        start=True,
-                        stop=True,
-                    )
-            grouped = work.tile([P, PASSES, P, PACK], BF16, align_bytes=64)
-            moved = grouped[:].rearrange("p c r t -> p (c r t)")
-            if tile_i < 4:
-                nc.vector.tensor_copy(out=moved, in_=o[:].rearrange("p c h r s u -> p (c h r s u)"))
-            else:
-                nc.scalar.copy(out=moved, in_=o[:].rearrange("p c h r s u -> p (c h r s u)"))
-            codes = keep.tile([P, PASSES, P], U32, name="y_codes%d" % tile_i, align_bytes=64)
-            scales = keep.tile([P, PASSES, P], U8, name="y_scales%d" % tile_i, align_bytes=64)
-            nc.vector.quantize_mx(
-                out=codes[:].rearrange("p c r -> p (c r)").bitcast(FP8X4),
-                scales=scales[:].rearrange("p c r -> p (c r)"),
-                in_=grouped[:].rearrange("p c r t -> p (c r t)"),
-            )
-            y_codes.append(codes)
-            y_scales.append(scales)
-
+        attn_sb, attn_T = {}, {}
+        v_sb, w_sb, shortcut_sb = {}, {}, {}
+        flipped_v, flipped_w, v_T, o_banks, grouped_y = {}, {}, {}, {}, {}
+        y_codes, y_scales, residual = {}, {}, {}
+        bias_all = keep.tile([P, C], BF16, name="bias_all")
         w_grouped = keep.tile([P, PASSES, C, PACK], BF16, name="w_grouped", align_bytes=64)
         w_codes = keep.tile([P, PASSES, C], U32, name="w_codes", align_bytes=64)
         w_scales = keep.tile([P, PASSES, C], U8, name="w_scales", align_bytes=64)
 
+        def spread_bias(half):
+            cols = slice(half * BANK, (half + 1) * BANK)
+            spread = psum.tile([P, BANK], F32, tag="acc", bufs=3, name="spread")
+            nc.tensor.matmul(spread[:], lhsT=ones[:], rhs=bias_rows[:, cols], start=True, stop=True)
+            nc.scalar.copy(out=bias_all[:, cols], in_=spread[:])
+
+        def transpose_attn(b):
+            flipped = psum.tile([P, HEADS, P], BF16, tag="flip", bufs=3, name="flip_a")
+            for g in range(HEADS):
+                nc.tensor.transpose(flipped[:, g, :], attn_sb[b][:, g, :], ident[:])
+            attn_T[b] = keep.tile([P, HEADS, P], BF16, name="attn_T%d" % b)
+            nc.scalar.copy(out=words(attn_T[b][:], "p g d -> p (g d)"), in_=words(flipped[:], "p g d -> p (g d)"))
+
+        def transpose_v(i):
+            flipped = psum.tile([P, 2, SIDE_CHUNKS, P], BF16, tag="flip", bufs=3, name="flip_v")
+            for h in range(2):
+                block = v_sb[i // 2][:, 2 * (i % 2) + h, :]
+                for s in range(SIDE_CHUNKS):
+                    nc.tensor.transpose(flipped[:, h, s, :], block[:, s * P : (s + 1) * P], ident[:])
+            flipped_v[i] = flipped
+
+        def copy_v(i):
+            v_T[i] = work.tile([P, 2, SIDE_CHUNKS, P], BF16, name="v_T")
+            nc.scalar.copy(
+                out=words(v_T[i][:], "p h s q -> p (h s q)"), in_=words(flipped_v[i][:], "p h s q -> p (h s q)")
+            )
+
+        def multiply(i):
+            o = psum.tile([P, PASSES, 2, HEAD_ROWS, PAIRS, SIDES], BF16, tag="o", bufs=2, name="o")
+            for h in range(2):
+                head = 2 * i + h
+                for c in range(PASSES):
+                    nc.tensor.matmul(
+                        o[:, c, h].rearrange("p r s u -> p s r u"),
+                        lhsT=attn_T[head // HEADS][:, head % HEADS, :],
+                        rhs=v_T[i][:, h, PAIRS * c : PAIRS * (c + 1), :].rearrange("p s (r u) -> p s r u", u=SIDES),
+                        start=True,
+                        stop=True,
+                    )
+            o_banks[i] = o
+
+        def copy_y(i):
+            grouped_y[i] = work.tile([P, PASSES, P, PACK], BF16, align_bytes=64, name="grouped")
+            nc.scalar.copy(
+                out=words(grouped_y[i][:], "p c r t -> p (c r t)"), in_=words(o_banks[i][:], "p c h r s u -> p (c h r s u)")
+            )
+
+        def quantise_y(i):
+            y_codes[i] = keep.tile([P, PASSES, P], U32, name="y_codes%d" % i, align_bytes=64)
+            y_scales[i] = keep.tile([P, PASSES, P], U8, name="y_scales%d" % i, align_bytes=64)
+            nc.vector.quantize_mx(
+                out=y_codes[i][:].rearrange("p c r -> p (c r)").bitcast(FP8X4),
+                scales=y_scales[i][:].rearrange("p c r -> p (c r)"),
+                in_=grouped_y[i][:].rearrange("p c r t -> p (c r t)"),
+            )
+
         def transpose_w(j_tile):
-            flipped = psum.tile([P, PASSES, P, PAIRS, SIDES], BF16, tag="flip", bufs=3)
+            flipped = psum.tile([P, PASSES, P, PAIRS, SIDES], BF16, tag="flip", bufs=3, name="flip_w")
             for i in range(2):
                 block = w_sb[j_tile // 2][:, 2 * (j_tile % 2) + i, :]
                 for c in range(PASSES):
@@ -145,70 +146,92 @@ def tile_transposedattentiontransformer_pb_kernel(tc, attn, v, w_proj, b_proj, s
                         nc.tensor.transpose(
                             flipped[:, c, i * HEAD_ROWS : (i + 1) * HEAD_ROWS, s, :], block[:, k0 : k0 + P], ident[:]
                         )
-            dst = w_grouped[:, :, j_tile * P : (j_tile + 1) * P, :].rearrange("p c j t -> p c (j t)").bitcast(F32)
-            moved = flipped[:].rearrange("p c j s u -> p c (j s u)").bitcast(F32)
-            if j_tile % 2 == 0:
-                nc.scalar.copy(out=dst, in_=moved)
-            else:
-                nc.vector.tensor_copy(out=dst, in_=moved)
+            flipped_w[j_tile] = flipped
 
-        def quantise_w(half):
+        def copy_w(j_tile, copy):
+            copy(
+                out=words(w_grouped[:, :, j_tile * P : (j_tile + 1) * P, :], "p c j t -> p c (j t)"),
+                in_=words(flipped_w[j_tile][:], "p c j s u -> p c (j s u)"),
+            )
+
+        def quantise_w(half, c):
             cols = slice(half * BANK, (half + 1) * BANK)
-            for c in range(PASSES):
-                nc.vector.quantize_mx(
-                    out=w_codes[:, c, cols].bitcast(FP8X4),
-                    scales=w_scales[:, c, cols],
-                    in_=w_grouped[:, c, cols, :].rearrange("p j t -> p (j t)"),
-                )
+            nc.vector.quantize_mx(
+                out=w_codes[:, c, cols].bitcast(FP8X4),
+                scales=w_scales[:, c, cols],
+                in_=w_grouped[:, c, cols, :].rearrange("p j t -> p (j t)"),
+            )
 
-        def second_stage(tile_i):
+        def add_bias(i, half, engine):
+            if half == 0:
+                residual[i] = keep.tile([P, C], F32, name="residual%d" % i)
+            cols = slice(half * BANK, (half + 1) * BANK)
+            engine.tensor_tensor(
+                out=residual[i][:, cols], in0=shortcut_sb[i // 2][:, i % 2, cols], in1=bias_all[:, cols], op=ADD
+            )
+
+        def project(i):
             for half in range(HALVES):
                 cols = slice(half * BANK, (half + 1) * BANK)
-                acc = psum.tile([P, BANK], F32, tag="acc", bufs=3)
+                acc = psum.tile([P, BANK], F32, tag="acc", bufs=3, name="acc")
                 for c in range(PASSES):
                     nc.tensor.matmul_mx(
                         out=acc[:],
-                        lhsT=y_codes[tile_i][:, c, :].bitcast(FP8X4),
-                        lhsT_scale=y_scales[tile_i][:, c, :],
+                        lhsT=y_codes[i][:, c, :].bitcast(FP8X4),
+                        lhsT_scale=y_scales[i][:, c, :],
                         rhs=w_codes[:, c, cols].bitcast(FP8X4),
                         rhs_scale=w_scales[:, c, cols],
                         start=(c == 0),
                         stop=(c == PASSES - 1),
                     )
-                nc.vector.tensor_tensor(out=residual[tile_i][:, cols], in0=acc[:], in1=residual[tile_i][:, cols], op=ADD)
-            nc.sync.dma_start(out=out_rows[tile_i * P : (tile_i + 1) * P, :], in_=residual[tile_i][:])
+                nc.vector.tensor_tensor(out=residual[i][:, cols], in0=acc[:], in1=residual[i][:, cols], op=ADD)
+            nc.sync.dma_start(out=out_rows[i * P : (i + 1) * P, :], in_=residual[i][:])
 
-        def first_stage_of_group(group):
-            if group % 2 == 0:
-                transpose_attn(group // 2)
-            first_stage(2 * group)
-            first_stage(2 * group + 1)
+        attn_sb[0] = load_attn(0)
+        v_sb[0] = load_four_blocks(v_halves, 0, "v_sb0")
+        nc.sync.dma_start(out=bias_rows[0:1, :], in_=b_proj.rearrange("(o c) -> o c", o=1))
+        w_sb[0] = load_four_blocks(w_halves, 0, "w_sb0")
+        v_sb[1] = load_four_blocks(v_halves, 1, "v_sb1")
+        w_sb[1] = load_four_blocks(w_halves, 1, "w_sb1")
+        shortcut_sb[0] = load_shortcut(0)
+        v_sb[2] = load_four_blocks(v_halves, 2, "v_sb2")
+        attn_sb[1] = load_attn(1)
+        w_sb[2] = load_four_blocks(w_halves, 2, "w_sb2")
+        shortcut_sb[1] = load_shortcut(1)
+        v_sb[3] = load_four_blocks(v_halves, 3, "v_sb3")
+        w_sb[3] = load_four_blocks(w_halves, 3, "w_sb3")
+        shortcut_sb[2] = load_shortcut(2)
+        shortcut_sb[3] = load_shortcut(3)
 
-        first_stage_of_group(0)
-        bias_all = keep.tile([P, C], BF16, name="bias_all")
-        for half in range(HALVES):
-            cols = slice(half * BANK, (half + 1) * BANK)
-            spread = psum.tile([P, BANK], F32, tag="acc", bufs=3)
-            nc.tensor.matmul(spread[:], lhsT=ones[:], rhs=bias_rows[:, cols], start=True, stop=True)
-            nc.scalar.copy(out=bias_all[:, cols], in_=spread[:])
-
-        residual = []
-        for tile_i in range(ROW_TILES):
-            summed = keep.tile([P, C], F32, name="residual%d" % tile_i)
+        with tc.manual_schedule():
+            transpose_attn(0)
+            for i in range(ROW_TILES + 2):
+                if i < ROW_TILES:
+                    if i == 4:
+                        transpose_attn(1)
+                    transpose_v(i)
+                    copy_v(i)
+                    transpose_w(i)
+                    copy_w(i, nc.vector.tensor_copy)
+                if i == 1:
+                    spread_bias(0)
+                    spread_bias(1)
+                if 1 <= i <= ROW_TILES:
+                    multiply(i - 1)
+                    copy_y(i - 1)
+                if i >= 2:
+                    quantise_y(i - 2)
+                if i == 4 or i == 8:
+                    quantise_w(i // 4 - 1, 0)
+                    quantise_w(i // 4 - 1, 1)
+                if 3 <= i <= 5:
+                    add_bias(i - 3, 0, nc.vector)
+                    add_bias(i - 3, 1, nc.vector)
+                if 6 <= i:
+                    for half in range(HALVES):
+                        if i - 3 < ROW_TILES:
+                            add_bias(i - 3, half, nc.gpsimd)
             for half in range(HALVES):
-                cols = slice(half * BANK, (half + 1) * BANK)
-                nc.gpsimd.tensor_tensor(
-                    out=summed[:, cols], in0=shortcut_sb[tile_i // 2][:, tile_i % 2, cols], in1=bias_all[:, cols], op=ADD
-                )
-            residual.append(summed)
-
-        first_stage_of_group(1)
-        for j_tile in range(ROW_TILES):
-            transpose_w(j_tile)
-            if j_tile % 4 == 3:
-                quantise_w(j_tile // 4)
-        for group in range(GROUPS):
-            second_stage(2 * group)
-            second_stage(2 * group + 1)
-            if group + 2 < GROUPS:
-                first_stage_of_group(group + 2)
+                add_bias(7, half, nc.gpsimd)
+            for i in range(ROW_TILES):
+                project(i)

@@ -68,13 +68,15 @@ def tile_transposedattentiontransformer_pb_kernel(tc, attn, v, w_proj, b_proj, s
         make_identity(nc, ident[:])
         ones = keep.tile([P, P], BF16, name="ones")
         nc.vector.memset(ones[:], 1.0)
+        zeros = keep.tile([P, BANK], BF16, name="zeros")
+        nc.vector.memset(zeros[:], 0.0)
         bias_rows = keep.tile([P, C], BF16, name="bias_rows")
         nc.vector.memset(bias_rows[:], 0.0)
 
         attn_sb, attn_T = {}, {}
         v_sb, w_sb, shortcut_sb = {}, {}, {}
         flipped_v, flipped_w, v_T, o_banks, grouped_y = {}, {}, {}, {}, {}
-        y_codes, y_scales, residual = {}, {}, {}
+        y_codes, y_scales, residual, banks = {}, {}, {}, {}
         bias_all = keep.tile([P, C], BF16, name="bias_all")
         w_grouped = keep.tile([P, PASSES, C, PACK], BF16, name="w_grouped", align_bytes=64)
         w_codes = keep.tile([P, PASSES, C], U32, name="w_codes", align_bytes=64)
@@ -170,68 +172,90 @@ def tile_transposedattentiontransformer_pb_kernel(tc, attn, v, w_proj, b_proj, s
                 out=residual[i][:, cols], in0=shortcut_sb[i // 2][:, i % 2, cols], in1=bias_all[:, cols], op=ADD
             )
 
-        def project(i):
-            for half in range(HALVES):
-                cols = slice(half * BANK, (half + 1) * BANK)
-                acc = psum.tile([P, BANK], F32, tag="acc", bufs=3, name="acc")
-                for c in range(PASSES):
-                    nc.tensor.matmul_mx(
-                        out=acc[:],
-                        lhsT=y_codes[i][:, c, :].bitcast(FP8X4),
-                        lhsT_scale=y_scales[i][:, c, :],
-                        rhs=w_codes[:, c, cols].bitcast(FP8X4),
-                        rhs_scale=w_scales[:, c, cols],
-                        start=(c == 0),
-                        stop=(c == PASSES - 1),
-                    )
-                nc.vector.tensor_tensor(out=residual[i][:, cols], in0=acc[:], in1=residual[i][:, cols], op=ADD)
-            nc.sync.dma_start(out=out_rows[i * P : (i + 1) * P, :], in_=residual[i][:])
+        def project(i, half):
+            cols = slice(half * BANK, (half + 1) * BANK)
+            acc = psum.tile([P, BANK], F32, tag="acc", bufs=3, name="acc")
+            for c in range(PASSES):
+                nc.tensor.matmul_mx(
+                    out=acc[:],
+                    lhsT=y_codes[i][:, c, :].bitcast(FP8X4),
+                    lhsT_scale=y_scales[i][:, c, :],
+                    rhs=w_codes[:, c, cols].bitcast(FP8X4),
+                    rhs_scale=w_scales[:, c, cols],
+                    start=(c == 0),
+                    stop=(c == PASSES - 1),
+                )
+            banks[i, half] = acc
+
+        def finish(i, half):
+            cols = slice(half * BANK, (half + 1) * BANK)
+            nc.vector.tensor_tensor(out=residual[i][:, cols], in0=banks[i, half][:], in1=residual[i][:, cols], op=ADD)
+            if half == 1:
+                nc.sync.dma_start(out=out_rows[i * P : (i + 1) * P, :], in_=residual[i][:])
 
         attn_sb[0] = load_attn(0)
-        v_sb[0] = load_four_blocks(v_halves, 0, "v_sb0")
         nc.sync.dma_start(out=bias_rows[0:1, :], in_=b_proj.rearrange("(o c) -> o c", o=1))
+        v_sb[0] = load_four_blocks(v_halves, 0, "v_sb0")
         w_sb[0] = load_four_blocks(w_halves, 0, "w_sb0")
-        v_sb[1] = load_four_blocks(v_halves, 1, "v_sb1")
         w_sb[1] = load_four_blocks(w_halves, 1, "w_sb1")
-        shortcut_sb[0] = load_shortcut(0)
-        v_sb[2] = load_four_blocks(v_halves, 2, "v_sb2")
-        attn_sb[1] = load_attn(1)
         w_sb[2] = load_four_blocks(w_halves, 2, "w_sb2")
-        shortcut_sb[1] = load_shortcut(1)
-        v_sb[3] = load_four_blocks(v_halves, 3, "v_sb3")
         w_sb[3] = load_four_blocks(w_halves, 3, "w_sb3")
+        shortcut_sb[0] = load_shortcut(0)
+        v_sb[1] = load_four_blocks(v_halves, 1, "v_sb1")
+        shortcut_sb[1] = load_shortcut(1)
+        attn_sb[1] = load_attn(1)
+        v_sb[2] = load_four_blocks(v_halves, 2, "v_sb2")
         shortcut_sb[2] = load_shortcut(2)
+        v_sb[3] = load_four_blocks(v_halves, 3, "v_sb3")
         shortcut_sb[3] = load_shortcut(3)
 
         with tc.manual_schedule():
+            for n in range(4):
+                warm = psum.tile([P, BANK], F32, tag="acc", bufs=3, name="warm")
+                nc.tensor.matmul(warm[:], lhsT=ones[:], rhs=zeros[:], start=True, stop=True)
             transpose_attn(0)
-            for i in range(ROW_TILES + 2):
-                if i < ROW_TILES:
-                    if i == 4:
+            spread_bias(0)
+            spread_bias(1)
+            transpose_v(0)
+            copy_v(0)
+            transpose_v(1)
+            copy_v(1)
+            for j in range(ROW_TILES):
+                transpose_w(j)
+                copy_w(j, nc.scalar.copy)
+                if j < 2:
+                    multiply(j)
+                    copy_y(j)
+                if 2 <= j < 4:
+                    quantise_y(j - 2)
+                if j == 4:
+                    quantise_w(0, 0)
+                    quantise_w(0, 1)
+                if j == 5:
+                    for k in range(2):
+                        add_bias(k, 0, nc.vector)
+                        add_bias(k, 1, nc.vector)
+            quantise_w(1, 0)
+            quantise_w(1, 1)
+            for g in range(GROUPS):
+                nxt = 2 * g + 2
+                if nxt < ROW_TILES:
+                    if nxt == 4:
                         transpose_attn(1)
-                    transpose_v(i)
-                    copy_v(i)
-                    transpose_w(i)
-                    copy_w(i, nc.vector.tensor_copy)
-                if i == 1:
-                    spread_bias(0)
-                    spread_bias(1)
-                if 1 <= i <= ROW_TILES:
-                    multiply(i - 1)
-                    copy_y(i - 1)
-                if i >= 2:
-                    quantise_y(i - 2)
-                if i == 4 or i == 8:
-                    quantise_w(i // 4 - 1, 0)
-                    quantise_w(i // 4 - 1, 1)
-                if 3 <= i <= 5:
-                    add_bias(i - 3, 0, nc.vector)
-                    add_bias(i - 3, 1, nc.vector)
-                if 6 <= i:
+                    transpose_v(nxt)
+                    copy_v(nxt)
+                    transpose_v(nxt + 1)
+                    copy_v(nxt + 1)
+                for k in range(2):
                     for half in range(HALVES):
-                        if i - 3 < ROW_TILES:
-                            add_bias(i - 3, half, nc.gpsimd)
-            for half in range(HALVES):
-                add_bias(7, half, nc.gpsimd)
-            for i in range(ROW_TILES):
-                project(i)
+                        project(2 * g + k, half)
+                        finish(2 * g + k, half)
+                    if nxt < ROW_TILES:
+                        multiply(nxt + k)
+                        copy_y(nxt + k)
+                        if k == 1:
+                            quantise_y(nxt)
+                        add_bias(nxt + k, 0, nc.vector)
+                        add_bias(nxt + k, 1, nc.vector)
+                if nxt < ROW_TILES:
+                    quantise_y(nxt + 1)

@@ -20,6 +20,7 @@ HEAD_ROWS = TOKENS // CHUNKS
 GROUPS = ROW_TILES // 2
 BANK = 512
 HALVES = C // BANK
+ATTN_ROWS = HEADS * P // P
 SIDES = 2
 HALF_ROW = C // SIDES
 SIDE_CHUNKS = CHUNKS // SIDES
@@ -57,9 +58,9 @@ def tile_transposedattentiontransformer_pb_kernel(tc, attn, v, w_proj, b_proj, s
             return pair
 
         def load_attn(b):
-            heads = keep.tile([P, HEADS, P], BF16, name="attn_sb%d" % b)
-            nc.sync.dma_start(out=heads[:], in_=attn[b].rearrange("g d e -> d g e"))
-            return heads
+            rows = keep.tile([P, ATTN_ROWS, P], BF16, name="attn_sb%d" % b)
+            nc.sync.dma_start(out=rows[:], in_=attn[b].rearrange("g (q i) e -> (g q) i e", i=ATTN_ROWS))
+            return rows
 
         def words(ap, merge):
             return ap.rearrange(merge).bitcast(F32)
@@ -89,11 +90,15 @@ def tile_transposedattentiontransformer_pb_kernel(tc, attn, v, w_proj, b_proj, s
             nc.scalar.copy(out=bias_all[:, cols], in_=spread[:])
 
         def transpose_attn(b):
-            flipped = psum.tile([P, HEADS, P], BF16, tag="flip", bufs=3, name="flip_a")
-            for g in range(HEADS):
-                nc.tensor.transpose(flipped[:, g, :], attn_sb[b][:, g, :], ident[:])
+            flipped = psum.tile([P, ATTN_ROWS, P], BF16, tag="flip", bufs=3, name="flip_a")
+            for i in range(ATTN_ROWS):
+                nc.tensor.transpose(flipped[:, i, :], attn_sb[b][:, i, :], ident[:])
             attn_T[b] = keep.tile([P, HEADS, P], BF16, name="attn_T%d" % b)
-            nc.scalar.copy(out=words(attn_T[b][:], "p g d -> p (g d)"), in_=words(flipped[:], "p g d -> p (g d)"))
+            for copy, heads in ((nc.scalar.copy, slice(0, HEADS // 2)), (nc.vector.tensor_copy, slice(HEADS // 2, HEADS))):
+                copy(
+                    out=attn_T[b][:, heads, :].rearrange("p g (q i) -> p (g q) i", i=ATTN_ROWS),
+                    in_=flipped[:].rearrange("p i (g q) -> p g q i", g=HEADS)[:, heads].rearrange("p g q i -> p (g q) i"),
+                )
 
         def transpose_v(i):
             flipped = psum.tile([P, 2, SIDE_CHUNKS, P], BF16, tag="flip", bufs=3, name="flip_v")
@@ -164,13 +169,14 @@ def tile_transposedattentiontransformer_pb_kernel(tc, attn, v, w_proj, b_proj, s
                 in_=w_grouped[:, c, cols, :].rearrange("p j t -> p (j t)"),
             )
 
-        def add_bias(i, half, engine):
-            if half == 0:
-                residual[i] = keep.tile([P, C], F32, name="residual%d" % i)
-            cols = slice(half * BANK, (half + 1) * BANK)
-            engine.tensor_tensor(
-                out=residual[i][:, cols], in0=shortcut_sb[i // 2][:, i % 2, cols], in1=bias_all[:, cols], op=ADD
-            )
+        def add_bias(i, engine, pieces=1):
+            residual[i] = keep.tile([P, C], F32, name="residual%d" % i)
+            width = C // pieces
+            for n in range(pieces):
+                cols = slice(n * width, (n + 1) * width)
+                engine.tensor_tensor(
+                    out=residual[i][:, cols], in0=shortcut_sb[i // 2][:, i % 2, cols], in1=bias_all[:, cols], op=ADD
+                )
 
         def project(i, half):
             cols = slice(half * BANK, (half + 1) * BANK)
@@ -190,7 +196,9 @@ def tile_transposedattentiontransformer_pb_kernel(tc, attn, v, w_proj, b_proj, s
         def finish(i, half):
             cols = slice(half * BANK, (half + 1) * BANK)
             nc.vector.tensor_tensor(out=residual[i][:, cols], in0=banks[i, half][:], in1=residual[i][:, cols], op=ADD)
-            if half == 1:
+            if i == ROW_TILES - 1:
+                nc.sync.dma_start(out=out_rows[i * P : (i + 1) * P, cols], in_=residual[i][:, cols])
+            elif half == 1:
                 nc.sync.dma_start(out=out_rows[i * P : (i + 1) * P, :], in_=residual[i][:])
 
         attn_sb[0] = load_attn(0)
@@ -198,64 +206,83 @@ def tile_transposedattentiontransformer_pb_kernel(tc, attn, v, w_proj, b_proj, s
         v_sb[0] = load_four_blocks(v_halves, 0, "v_sb0")
         w_sb[0] = load_four_blocks(w_halves, 0, "w_sb0")
         w_sb[1] = load_four_blocks(w_halves, 1, "w_sb1")
-        w_sb[2] = load_four_blocks(w_halves, 2, "w_sb2")
-        w_sb[3] = load_four_blocks(w_halves, 3, "w_sb3")
         shortcut_sb[0] = load_shortcut(0)
         v_sb[1] = load_four_blocks(v_halves, 1, "v_sb1")
-        shortcut_sb[1] = load_shortcut(1)
+        w_sb[2] = load_four_blocks(w_halves, 2, "w_sb2")
+        w_sb[3] = load_four_blocks(w_halves, 3, "w_sb3")
         attn_sb[1] = load_attn(1)
         v_sb[2] = load_four_blocks(v_halves, 2, "v_sb2")
-        shortcut_sb[2] = load_shortcut(2)
+        shortcut_sb[1] = load_shortcut(1)
         v_sb[3] = load_four_blocks(v_halves, 3, "v_sb3")
+        shortcut_sb[2] = load_shortcut(2)
         shortcut_sb[3] = load_shortcut(3)
 
         with tc.manual_schedule():
             for n in range(4):
                 warm = psum.tile([P, BANK], F32, tag="acc", bufs=3, name="warm")
                 nc.tensor.matmul(warm[:], lhsT=ones[:], rhs=zeros[:], start=True, stop=True)
+
+            def early(i):
+                transpose_v(i)
+                copy_v(i)
+
+            def middle(i):
+                multiply(i)
+                copy_y(i)
+
+            def weights(j):
+                transpose_w(j)
+                copy_w(j, nc.vector.tensor_copy if j % 4 == 1 else nc.scalar.copy)
+
             transpose_attn(0)
+            early(0)
+            early(1)
             spread_bias(0)
             spread_bias(1)
-            transpose_v(0)
-            copy_v(0)
-            transpose_v(1)
-            copy_v(1)
-            for j in range(ROW_TILES):
-                transpose_w(j)
-                copy_w(j, nc.scalar.copy)
-                if j < 2:
-                    multiply(j)
-                    copy_y(j)
-                if 2 <= j < 4:
-                    quantise_y(j - 2)
-                if j == 4:
-                    quantise_w(0, 0)
-                    quantise_w(0, 1)
-                if j == 5:
-                    for k in range(2):
-                        add_bias(k, 0, nc.vector)
-                        add_bias(k, 1, nc.vector)
+            for i in range(ROW_TILES):
+                add_bias(i, nc.gpsimd, 2)
+            weights(0)
+            middle(0)
+            weights(1)
+            middle(1)
+            quantise_y(0)
+            weights(2)
+            quantise_y(1)
+            weights(3)
+            early(2)
+            early(3)
+            weights(4)
+            middle(2)
+            quantise_w(0, 0)
+            quantise_w(0, 1)
+            weights(5)
+            middle(3)
+            quantise_y(2)
+            weights(6)
+            quantise_y(3)
+            weights(7)
             quantise_w(1, 0)
             quantise_w(1, 1)
             for g in range(GROUPS):
-                nxt = 2 * g + 2
-                if nxt < ROW_TILES:
-                    if nxt == 4:
-                        transpose_attn(1)
-                    transpose_v(nxt)
-                    copy_v(nxt)
-                    transpose_v(nxt + 1)
-                    copy_v(nxt + 1)
-                for k in range(2):
-                    for half in range(HALVES):
-                        project(2 * g + k, half)
-                        finish(2 * g + k, half)
-                    if nxt < ROW_TILES:
-                        multiply(nxt + k)
-                        copy_y(nxt + k)
-                        if k == 1:
-                            quantise_y(nxt)
-                        add_bias(nxt + k, 0, nc.vector)
-                        add_bias(nxt + k, 1, nc.vector)
-                if nxt < ROW_TILES:
+                nxt = 2 * g + 4
+                more = nxt < ROW_TILES
+                if nxt == 4:
+                    transpose_attn(1)
+                if more:
+                    early(nxt)
+                    early(nxt + 1)
+                project(2 * g, 0)
+                finish(2 * g, 0)
+                if more:
+                    middle(nxt)
+                project(2 * g, 1)
+                finish(2 * g, 1)
+                if more:
+                    quantise_y(nxt)
+                    middle(nxt + 1)
+                project(2 * g + 1, 0)
+                finish(2 * g + 1, 0)
+                if more:
                     quantise_y(nxt + 1)
+                project(2 * g + 1, 1)
+                finish(2 * g + 1, 1)

@@ -41,13 +41,12 @@ def tile_transposedattentiontransformer_pb_kernel(tc, attn, v, w_proj, b_proj, s
         work = ctx.enter_context(tc.tile_pool(name="work", bufs=3))
         psum = ctx.enter_context(tc.psum_pool(name="psum", bufs=1))
 
-        def load_four_blocks(halves, group, name):
-            four = keep.tile([P, 2 * SIDES, HALF_ROW], BF16, name=name)
-            nc.sync.dma_start(
-                out=four[:],
-                in_=halves[4 * P * group : 4 * P * (group + 1), :].rearrange("(i p) x -> p i x", p=P),
-            )
-            return four
+        def load_blocks(halves, tiles, into, name):
+            start, stop = 2 * P * tiles[0], 2 * P * (tiles[-1] + 1)
+            blocks = keep.tile([P, 2 * len(tiles), HALF_ROW], BF16, name="%s%d" % (name, tiles[0]))
+            nc.sync.dma_start(out=blocks[:], in_=halves[start:stop, :].rearrange("(i p) x -> p i x", p=P))
+            for n, i in enumerate(tiles):
+                into[i] = blocks[:, 2 * n : 2 * n + 2, :]
 
         def load_shortcut(group):
             pair = keep.tile([P, 2, C], BF16, name="shortcut_sb%d" % group)
@@ -65,12 +64,12 @@ def tile_transposedattentiontransformer_pb_kernel(tc, attn, v, w_proj, b_proj, s
         def words(ap, merge):
             return ap.rearrange(merge).bitcast(F32)
 
+        zeros = keep.tile([P, BANK], BF16, name="zeros")
+        nc.vector.memset(zeros[:], 0.0)
         ident = keep.tile([P, P], BF16, name="ident")
         make_identity(nc, ident[:])
         ones = keep.tile([P, P], BF16, name="ones")
         nc.vector.memset(ones[:], 1.0)
-        zeros = keep.tile([P, BANK], BF16, name="zeros")
-        nc.vector.memset(zeros[:], 0.0)
         bias_rows = keep.tile([P, C], BF16, name="bias_rows")
         nc.vector.memset(bias_rows[:], 0.0)
 
@@ -103,7 +102,7 @@ def tile_transposedattentiontransformer_pb_kernel(tc, attn, v, w_proj, b_proj, s
         def transpose_v(i):
             flipped = psum.tile([P, 2, SIDE_CHUNKS, P], BF16, tag="flip", bufs=3, name="flip_v")
             for h in range(2):
-                block = v_sb[i // 2][:, 2 * (i % 2) + h, :]
+                block = v_sb[i][:, h, :]
                 for s in range(SIDE_CHUNKS):
                     nc.tensor.transpose(flipped[:, h, s, :], block[:, s * P : (s + 1) * P], ident[:])
             flipped_v[i] = flipped
@@ -114,19 +113,18 @@ def tile_transposedattentiontransformer_pb_kernel(tc, attn, v, w_proj, b_proj, s
                 out=words(v_T[i][:], "p h s q -> p (h s q)"), in_=words(flipped_v[i][:], "p h s q -> p (h s q)")
             )
 
-        def multiply(i):
-            o = psum.tile([P, PASSES, 2, HEAD_ROWS, PAIRS, SIDES], BF16, tag="o", bufs=2, name="o")
-            for h in range(2):
-                head = 2 * i + h
-                for c in range(PASSES):
-                    nc.tensor.matmul(
-                        o[:, c, h].rearrange("p r s u -> p s r u"),
-                        lhsT=attn_T[head // HEADS][:, head % HEADS, :],
-                        rhs=v_T[i][:, h, PAIRS * c : PAIRS * (c + 1), :].rearrange("p s (r u) -> p s r u", u=SIDES),
-                        start=True,
-                        stop=True,
-                    )
-            o_banks[i] = o
+        def multiply(i, h):
+            if h == 0:
+                o_banks[i] = psum.tile([P, PASSES, 2, HEAD_ROWS, PAIRS, SIDES], BF16, tag="o", bufs=2, name="o")
+            head = 2 * i + h
+            for c in range(PASSES):
+                nc.tensor.matmul(
+                    o_banks[i][:, c, h].rearrange("p r s u -> p s r u"),
+                    lhsT=attn_T[head // HEADS][:, head % HEADS, :],
+                    rhs=v_T[i][:, h, PAIRS * c : PAIRS * (c + 1), :].rearrange("p s (r u) -> p s r u", u=SIDES),
+                    start=True,
+                    stop=True,
+                )
 
         def copy_y(i):
             grouped_y[i] = work.tile([P, PASSES, P, PACK], BF16, align_bytes=64, name="grouped")
@@ -146,7 +144,7 @@ def tile_transposedattentiontransformer_pb_kernel(tc, attn, v, w_proj, b_proj, s
         def transpose_w(j_tile):
             flipped = psum.tile([P, PASSES, P, PAIRS, SIDES], BF16, tag="flip", bufs=3, name="flip_w")
             for i in range(2):
-                block = w_sb[j_tile // 2][:, 2 * (j_tile % 2) + i, :]
+                block = w_sb[j_tile][:, i, :]
                 for c in range(PASSES):
                     for s in range(PAIRS):
                         k0 = (c * PAIRS + s) * P
@@ -202,37 +200,34 @@ def tile_transposedattentiontransformer_pb_kernel(tc, attn, v, w_proj, b_proj, s
                 nc.sync.dma_start(out=out_rows[i * P : (i + 1) * P, :], in_=residual[i][:])
 
         attn_sb[0] = load_attn(0)
+        load_blocks(v_halves, (0,), v_sb, "v_sb")
+        load_blocks(v_halves, (1,), v_sb, "v_sb")
+        load_blocks(w_halves, (0, 1), w_sb, "w_sb")
         nc.sync.dma_start(out=bias_rows[0:1, :], in_=b_proj.rearrange("(o c) -> o c", o=1))
-        v_sb[0] = load_four_blocks(v_halves, 0, "v_sb0")
-        w_sb[0] = load_four_blocks(w_halves, 0, "w_sb0")
-        w_sb[1] = load_four_blocks(w_halves, 1, "w_sb1")
         shortcut_sb[0] = load_shortcut(0)
-        v_sb[1] = load_four_blocks(v_halves, 1, "v_sb1")
-        w_sb[2] = load_four_blocks(w_halves, 2, "w_sb2")
-        w_sb[3] = load_four_blocks(w_halves, 3, "w_sb3")
+        load_blocks(w_halves, (2, 3), w_sb, "w_sb")
+        load_blocks(v_halves, (2, 3), v_sb, "v_sb")
+        load_blocks(w_halves, (4, 5), w_sb, "w_sb")
+        load_blocks(w_halves, (6, 7), w_sb, "w_sb")
         attn_sb[1] = load_attn(1)
-        v_sb[2] = load_four_blocks(v_halves, 2, "v_sb2")
+        load_blocks(v_halves, (4, 5), v_sb, "v_sb")
         shortcut_sb[1] = load_shortcut(1)
-        v_sb[3] = load_four_blocks(v_halves, 3, "v_sb3")
         shortcut_sb[2] = load_shortcut(2)
+        load_blocks(v_halves, (6, 7), v_sb, "v_sb")
         shortcut_sb[3] = load_shortcut(3)
 
         with tc.manual_schedule():
-            for n in range(4):
+            for n in range(3):
                 warm = psum.tile([P, BANK], F32, tag="acc", bufs=3, name="warm")
-                nc.tensor.matmul(warm[:], lhsT=ones[:], rhs=zeros[:], start=True, stop=True)
+                nc.tensor.matmul(warm[:], lhsT=zeros[:, :P], rhs=zeros[:], start=True, stop=True)
 
             def early(i):
                 transpose_v(i)
                 copy_v(i)
 
-            def middle(i):
-                multiply(i)
-                copy_y(i)
-
             def weights(j):
                 transpose_w(j)
-                copy_w(j, nc.vector.tensor_copy if j % 4 == 1 else nc.scalar.copy)
+                copy_w(j, nc.vector.tensor_copy if j % 2 else nc.scalar.copy)
 
             transpose_attn(0)
             early(0)
@@ -242,25 +237,33 @@ def tile_transposedattentiontransformer_pb_kernel(tc, attn, v, w_proj, b_proj, s
             for i in range(ROW_TILES):
                 add_bias(i, nc.gpsimd, 2)
             weights(0)
-            middle(0)
+            multiply(0, 0)
             weights(1)
-            middle(1)
-            quantise_y(0)
+            multiply(0, 1)
+            copy_y(0)
             weights(2)
-            quantise_y(1)
+            multiply(1, 0)
             weights(3)
             early(2)
+            multiply(1, 1)
+            copy_y(1)
+            quantise_y(0)
             early(3)
+            quantise_y(1)
             weights(4)
-            middle(2)
+            multiply(2, 0)
             quantise_w(0, 0)
             quantise_w(0, 1)
             weights(5)
-            middle(3)
-            quantise_y(2)
+            multiply(2, 1)
+            copy_y(2)
             weights(6)
-            quantise_y(3)
+            multiply(3, 0)
+            quantise_y(2)
             weights(7)
+            multiply(3, 1)
+            copy_y(3)
+            quantise_y(3)
             quantise_w(1, 0)
             quantise_w(1, 1)
             for g in range(GROUPS):
@@ -271,18 +274,12 @@ def tile_transposedattentiontransformer_pb_kernel(tc, attn, v, w_proj, b_proj, s
                 if more:
                     early(nxt)
                     early(nxt + 1)
-                project(2 * g, 0)
-                finish(2 * g, 0)
-                if more:
-                    middle(nxt)
-                project(2 * g, 1)
-                finish(2 * g, 1)
-                if more:
-                    quantise_y(nxt)
-                    middle(nxt + 1)
-                project(2 * g + 1, 0)
-                finish(2 * g + 1, 0)
-                if more:
-                    quantise_y(nxt + 1)
-                project(2 * g + 1, 1)
-                finish(2 * g + 1, 1)
+                for n, (k, half) in enumerate([(0, 0), (0, 1), (1, 0), (1, 1)]):
+                    project(2 * g + k, half)
+                    finish(2 * g + k, half)
+                    if more and n < 2:
+                        multiply(nxt + n, 0)
+                        multiply(nxt + n, 1)
+                        copy_y(nxt + n)
+                    if more and 1 <= n < 3:
+                        quantise_y(nxt + n - 1)

@@ -204,14 +204,14 @@ def tile_transposedattentiontransformer_pb_kernel(tc, attn, v, w_proj, b_proj, s
         load_blocks(v_halves, (1,), v_sb, "v_sb")
         load_blocks(w_halves, (0, 1), w_sb, "w_sb")
         nc.sync.dma_start(out=bias_rows[0:1, :], in_=b_proj.rearrange("(o c) -> o c", o=1))
-        shortcut_sb[0] = load_shortcut(0)
         load_blocks(w_halves, (2, 3), w_sb, "w_sb")
+        shortcut_sb[0] = load_shortcut(0)
         load_blocks(v_halves, (2, 3), v_sb, "v_sb")
         load_blocks(w_halves, (4, 5), w_sb, "w_sb")
         load_blocks(w_halves, (6, 7), w_sb, "w_sb")
+        shortcut_sb[1] = load_shortcut(1)
         attn_sb[1] = load_attn(1)
         load_blocks(v_halves, (4, 5), v_sb, "v_sb")
-        shortcut_sb[1] = load_shortcut(1)
         shortcut_sb[2] = load_shortcut(2)
         load_blocks(v_halves, (6, 7), v_sb, "v_sb")
         shortcut_sb[3] = load_shortcut(3)
@@ -234,13 +234,14 @@ def tile_transposedattentiontransformer_pb_kernel(tc, attn, v, w_proj, b_proj, s
             early(1)
             spread_bias(0)
             spread_bias(1)
-            for i in range(ROW_TILES):
+            for i in range(2, ROW_TILES):
                 add_bias(i, nc.gpsimd, 2)
             weights(0)
             multiply(0, 0)
             weights(1)
             multiply(0, 1)
             copy_y(0)
+            add_bias(0, nc.vector)
             weights(2)
             multiply(1, 0)
             weights(3)
@@ -248,6 +249,7 @@ def tile_transposedattentiontransformer_pb_kernel(tc, attn, v, w_proj, b_proj, s
             multiply(1, 1)
             copy_y(1)
             quantise_y(0)
+            add_bias(1, nc.vector)
             early(3)
             quantise_y(1)
             weights(4)

@@ -115,21 +115,19 @@ def tile_transposedattentiontransformer_pb_kernel(tc, attn, v, w_proj, b_proj, s
 
         def multiply(i, h):
             if h == 0:
-                o_banks[i] = psum.tile([P, PASSES, 2, HEAD_ROWS, PAIRS, SIDES], BF16, tag="o", bufs=2, name="o")
+                o_banks[i] = psum.tile([P, SIDE_CHUNKS, 2, P], BF16, tag="o", bufs=2, name="o")
             head = 2 * i + h
-            for c in range(PASSES):
-                nc.tensor.matmul(
-                    o_banks[i][:, c, h].rearrange("p r s u -> p s r u"),
-                    lhsT=attn_T[head // HEADS][:, head % HEADS, :],
-                    rhs=v_T[i][:, h, PAIRS * c : PAIRS * (c + 1), :].rearrange("p s (r u) -> p s r u", u=SIDES),
-                    start=True,
-                    stop=True,
-                )
+            nc.tensor.matmul(
+                o_banks[i][:, :, h, :], lhsT=attn_T[head // HEADS][:, head % HEADS, :], rhs=v_T[i][:, h], start=True, stop=True
+            )
 
         def copy_y(i):
             grouped_y[i] = work.tile([P, PASSES, P, PACK], BF16, align_bytes=64, name="grouped")
             nc.scalar.copy(
-                out=words(grouped_y[i][:], "p c r t -> p (c r t)"), in_=words(o_banks[i][:], "p c h r s u -> p (c h r s u)")
+                out=grouped_y[i][:].rearrange("p c r t -> p c (r t)").bitcast(F32).rearrange("p c (r s) -> p c r s", s=PAIRS),
+                in_=o_banks[i][:].rearrange("p s h q -> p (s h q)").bitcast(F32).rearrange(
+                    "p (c s r) -> p c r s", c=PASSES, s=PAIRS
+                ),
             )
 
         def quantise_y(i):
@@ -142,21 +140,20 @@ def tile_transposedattentiontransformer_pb_kernel(tc, attn, v, w_proj, b_proj, s
             )
 
         def transpose_w(j_tile):
-            flipped = psum.tile([P, PASSES, P, PAIRS, SIDES], BF16, tag="flip", bufs=3, name="flip_w")
+            flipped = psum.tile([P, SIDE_CHUNKS, 2, P], BF16, tag="flip", bufs=3, name="flip_w")
             for i in range(2):
-                block = w_sb[j_tile][:, i, :]
-                for c in range(PASSES):
-                    for s in range(PAIRS):
-                        k0 = (c * PAIRS + s) * P
-                        nc.tensor.transpose(
-                            flipped[:, c, i * HEAD_ROWS : (i + 1) * HEAD_ROWS, s, :], block[:, k0 : k0 + P], ident[:]
-                        )
+                for s in range(SIDE_CHUNKS):
+                    nc.tensor.transpose(flipped[:, s, i, :], w_sb[j_tile][:, i, s * P : (s + 1) * P], ident[:])
             flipped_w[j_tile] = flipped
 
         def copy_w(j_tile, copy):
             copy(
-                out=words(w_grouped[:, :, j_tile * P : (j_tile + 1) * P, :], "p c j t -> p c (j t)"),
-                in_=words(flipped_w[j_tile][:], "p c j s u -> p c (j s u)"),
+                out=w_grouped[:, :, j_tile * P : (j_tile + 1) * P, :].rearrange("p c j t -> p c (j t)").bitcast(F32).rearrange(
+                    "p c (j s) -> p c j s", s=PAIRS
+                ),
+                in_=flipped_w[j_tile][:].rearrange("p s i q -> p (s i q)").bitcast(F32).rearrange(
+                    "p (c s j) -> p c j s", c=PASSES, s=PAIRS
+                ),
             )
 
         def quantise_w(half, c):

@@ -191,10 +191,7 @@ def tile_transposedattentiontransformer_pb_kernel(tc, attn, v, w_proj, b_proj, s
         def finish(i, half):
             cols = slice(half * BANK, (half + 1) * BANK)
             nc.vector.tensor_tensor(out=residual[i][:, cols], in0=banks[i, half][:], in1=residual[i][:, cols], op=ADD)
-            if i == ROW_TILES - 1:
-                nc.sync.dma_start(out=out_rows[i * P : (i + 1) * P, cols], in_=residual[i][:, cols])
-            elif half == 1:
-                nc.sync.dma_start(out=out_rows[i * P : (i + 1) * P, :], in_=residual[i][:])
+            nc.sync.dma_start(out=out_rows[i * P : (i + 1) * P, cols], in_=residual[i][:, cols])
 
         attn_sb[0] = load_attn(0)
         load_blocks(v_halves, (0,), v_sb, "v_sb")
@@ -209,8 +206,8 @@ def tile_transposedattentiontransformer_pb_kernel(tc, attn, v, w_proj, b_proj, s
         shortcut_sb[1] = load_shortcut(1)
         attn_sb[1] = load_attn(1)
         load_blocks(v_halves, (4, 5), v_sb, "v_sb")
-        shortcut_sb[2] = load_shortcut(2)
         load_blocks(v_halves, (6, 7), v_sb, "v_sb")
+        shortcut_sb[2] = load_shortcut(2)
         shortcut_sb[3] = load_shortcut(3)
 
         with tc.manual_schedule():
@@ -224,7 +221,19 @@ def tile_transposedattentiontransformer_pb_kernel(tc, attn, v, w_proj, b_proj, s
 
             def weights(j):
                 transpose_w(j)
-                copy_w(j, nc.vector.tensor_copy if j % 2 else nc.scalar.copy)
+                copy_w(j, nc.vector.tensor_copy if j % 4 == 1 else nc.scalar.copy)
+
+            def middle(i):
+                multiply(i, 0)
+                multiply(i, 1)
+                copy_y(i)
+
+            def next_bank():
+                i, half = banks_left.pop(0)
+                project(i, half)
+                finish(i, half)
+
+            banks_left = [(0, 0), (1, 0), (0, 1), (1, 1)] + [(i, half) for i in range(2, ROW_TILES) for half in range(HALVES)]
 
             transpose_attn(0)
             early(0)
@@ -238,7 +247,6 @@ def tile_transposedattentiontransformer_pb_kernel(tc, attn, v, w_proj, b_proj, s
             weights(1)
             multiply(0, 1)
             copy_y(0)
-            add_bias(0, nc.vector)
             weights(2)
             multiply(1, 0)
             weights(3)
@@ -246,39 +254,41 @@ def tile_transposedattentiontransformer_pb_kernel(tc, attn, v, w_proj, b_proj, s
             multiply(1, 1)
             copy_y(1)
             quantise_y(0)
-            add_bias(1, nc.vector)
+            add_bias(0, nc.vector)
+            quantise_w(0, 0)
+            quantise_w(0, 1)
             early(3)
             quantise_y(1)
             weights(4)
             multiply(2, 0)
-            quantise_w(0, 0)
-            quantise_w(0, 1)
             weights(5)
             multiply(2, 1)
             copy_y(2)
+            add_bias(1, nc.vector)
             weights(6)
-            multiply(3, 0)
             quantise_y(2)
+            next_bank()
+            multiply(3, 0)
             weights(7)
+            next_bank()
             multiply(3, 1)
             copy_y(3)
-            quantise_y(3)
             quantise_w(1, 0)
             quantise_w(1, 1)
-            for g in range(GROUPS):
-                nxt = 2 * g + 4
-                more = nxt < ROW_TILES
-                if nxt == 4:
-                    transpose_attn(1)
-                if more:
-                    early(nxt)
-                    early(nxt + 1)
-                for n, (k, half) in enumerate([(0, 0), (0, 1), (1, 0), (1, 1)]):
-                    project(2 * g + k, half)
-                    finish(2 * g + k, half)
-                    if more and n < 2:
-                        multiply(nxt + n, 0)
-                        multiply(nxt + n, 1)
-                        copy_y(nxt + n)
-                    if more and 1 <= n < 3:
-                        quantise_y(nxt + n - 1)
+            quantise_y(3)
+            transpose_attn(1)
+            for pair in range(4, ROW_TILES, 2):
+                early(pair)
+                early(pair + 1)
+                next_bank()
+                next_bank()
+                middle(pair)
+                next_bank()
+                quantise_y(pair)
+                middle(pair + 1)
+                next_bank()
+                quantise_y(pair + 1)
+                next_bank()
+                next_bank()
+            while banks_left:
+                next_bank()

@@ -31,10 +31,10 @@ FLOPS = 2 * BATCH * HEADS * P * P * TOKENS + 2 * BATCH * TOKENS * C * C
 
 def tile_transposedattentiontransformer_pb_kernel(tc, attn, v, w_proj, b_proj, shortcut, out):
     nc = tc.nc
-    v_halves = v.flatten_outer_dims().rearrange("(q s) e -> q (s e)", s=SIDE_CHUNKS)
+    v_pairs = v.flatten_outer_dims().rearrange("(g p i s) e -> g p i (s e)", p=P, i=2, s=CHUNKS)
+    shortcut_pairs = shortcut.flatten_outer_dims().rearrange("(g p i) c -> g p i c", p=P, i=2)
+    out_pairs = out.flatten_outer_dims().rearrange("(g p i) c -> g p i c", p=P, i=2)
     w_halves = w_proj.rearrange("j (u k) -> (j u) k", u=SIDES)
-    shortcut_rows = shortcut.flatten_outer_dims()
-    out_rows = out.flatten_outer_dims()
 
     with ExitStack() as ctx:
         keep = ctx.enter_context(tc.tile_pool(name="keep", bufs=1))
@@ -48,12 +48,16 @@ def tile_transposedattentiontransformer_pb_kernel(tc, attn, v, w_proj, b_proj, s
             for n, i in enumerate(tiles):
                 into[i] = blocks[:, 2 * n : 2 * n + 2, :]
 
+        def load_v(tiles):
+            group, start = tiles[0] // 2, tiles[0] % 2
+            rows = keep.tile([P, len(tiles), C], BF16, name="v_sb%d" % tiles[0])
+            nc.sync.dma_start(out=rows[:], in_=v_pairs[group, :, start : start + len(tiles), :])
+            for n, i in enumerate(tiles):
+                v_sb[i] = rows[:, n, :]
+
         def load_shortcut(group):
             pair = keep.tile([P, 2, C], BF16, name="shortcut_sb%d" % group)
-            nc.sync.dma_start(
-                out=pair[:],
-                in_=shortcut_rows[2 * P * group : 2 * P * (group + 1), :].rearrange("(i p) c -> p i c", p=P),
-            )
+            nc.sync.dma_start(out=pair[:], in_=shortcut_pairs[group])
             return pair
 
         def load_attn(b):
@@ -100,35 +104,30 @@ def tile_transposedattentiontransformer_pb_kernel(tc, attn, v, w_proj, b_proj, s
                 )
 
         def transpose_v(i):
-            flipped = psum.tile([P, 2, SIDE_CHUNKS, P], BF16, tag="flip", bufs=3, name="flip_v")
-            for h in range(2):
-                block = v_sb[i][:, h, :]
-                for s in range(SIDE_CHUNKS):
-                    nc.tensor.transpose(flipped[:, h, s, :], block[:, s * P : (s + 1) * P], ident[:])
+            flipped = psum.tile([P, CHUNKS, P], BF16, tag="flip", bufs=3, name="flip_v")
+            for s in range(CHUNKS):
+                nc.tensor.transpose(flipped[:, s, :], v_sb[i][:, s * P : (s + 1) * P], ident[:])
             flipped_v[i] = flipped
 
         def copy_v(i):
-            v_T[i] = work.tile([P, 2, SIDE_CHUNKS, P], BF16, name="v_T")
-            nc.scalar.copy(
-                out=words(v_T[i][:], "p h s q -> p (h s q)"), in_=words(flipped_v[i][:], "p h s q -> p (h s q)")
-            )
+            v_T[i] = work.tile([P, CHUNKS, P], BF16, name="v_T")
+            nc.scalar.copy(out=words(v_T[i][:], "p s r -> p (s r)"), in_=words(flipped_v[i][:], "p s r -> p (s r)"))
 
-        def multiply(i, h):
-            if h == 0:
-                o_banks[i] = psum.tile([P, SIDE_CHUNKS, 2, P], BF16, tag="o", bufs=2, name="o")
-            head = 2 * i + h
-            nc.tensor.matmul(
-                o_banks[i][:, :, h, :], lhsT=attn_T[head // HEADS][:, head % HEADS, :], rhs=v_T[i][:, h], start=True, stop=True
-            )
+        def multiply(i, part):
+            if part == 0:
+                o_banks[i] = psum.tile([P, CHUNKS, P], BF16, tag="o", bufs=2, name="o")
+            for n in (2 * part, 2 * part + 1):
+                head = 4 * (i // 2) + n
+                rows = slice(n * P // 4, (n + 1) * P // 4)
+                nc.tensor.matmul(
+                    o_banks[i][:, :, rows], lhsT=attn_T[head // HEADS][:, head % HEADS, :], rhs=v_T[i][:, :, rows], start=True, stop=True
+                )
 
         def copy_y(i):
             grouped_y[i] = work.tile([P, PASSES, P, PACK], BF16, align_bytes=64, name="grouped")
-            nc.scalar.copy(
-                out=grouped_y[i][:].rearrange("p c r t -> p c (r t)").bitcast(F32).rearrange("p c (r s) -> p c r s", s=PAIRS),
-                in_=o_banks[i][:].rearrange("p s h q -> p (s h q)").bitcast(F32).rearrange(
-                    "p (c s r) -> p c r s", c=PASSES, s=PAIRS
-                ),
-            )
+            chunks = o_banks[i][:].rearrange("p (u c s) r -> p c r s u", u=SIDES, c=PASSES)
+            for c in range(PASSES):
+                nc.scalar.copy(out=grouped_y[i][:, c].rearrange("p r (s u) -> p r s u", u=SIDES), in_=chunks[:, c])
 
         def quantise_y(i):
             y_codes[i] = keep.tile([P, PASSES, P], U32, name="y_codes%d" % i, align_bytes=64)
@@ -191,22 +190,25 @@ def tile_transposedattentiontransformer_pb_kernel(tc, attn, v, w_proj, b_proj, s
         def finish(i, half):
             cols = slice(half * BANK, (half + 1) * BANK)
             nc.vector.tensor_tensor(out=residual[i][:, cols], in0=banks[i, half][:], in1=residual[i][:, cols], op=ADD)
-            nc.sync.dma_start(out=out_rows[i * P : (i + 1) * P, cols], in_=residual[i][:, cols])
+            if i >= ROW_TILES - 2:
+                nc.sync.dma_start(out=out_pairs[i // 2, :, i % 2, cols], in_=residual[i][:, cols])
+            elif half == 1:
+                nc.sync.dma_start(out=out_pairs[i // 2, :, i % 2, :], in_=residual[i][:])
 
         attn_sb[0] = load_attn(0)
-        load_blocks(v_halves, (0,), v_sb, "v_sb")
-        load_blocks(v_halves, (1,), v_sb, "v_sb")
+        load_v((0,))
+        load_v((1,))
         load_blocks(w_halves, (0, 1), w_sb, "w_sb")
         nc.sync.dma_start(out=bias_rows[0:1, :], in_=b_proj.rearrange("(o c) -> o c", o=1))
         load_blocks(w_halves, (2, 3), w_sb, "w_sb")
         shortcut_sb[0] = load_shortcut(0)
-        load_blocks(v_halves, (2, 3), v_sb, "v_sb")
+        load_v((2, 3))
         load_blocks(w_halves, (4, 5), w_sb, "w_sb")
         load_blocks(w_halves, (6, 7), w_sb, "w_sb")
         shortcut_sb[1] = load_shortcut(1)
         attn_sb[1] = load_attn(1)
-        load_blocks(v_halves, (4, 5), v_sb, "v_sb")
-        load_blocks(v_halves, (6, 7), v_sb, "v_sb")
+        load_v((4, 5))
+        load_v((6, 7))
         shortcut_sb[2] = load_shortcut(2)
         shortcut_sb[3] = load_shortcut(3)
 

@@ -21,10 +21,6 @@ GROUPS = ROW_TILES // 2
 BANK = 512
 HALVES = C // BANK
 ATTN_ROWS = HEADS * P // P
-SIDES = 2
-HALF_ROW = C // SIDES
-SIDE_CHUNKS = CHUNKS // SIDES
-PAIRS = PACK // SIDES
 
 FLOPS = 2 * BATCH * HEADS * P * P * TOKENS + 2 * BATCH * TOKENS * C * C
 
@@ -34,19 +30,19 @@ def tile_transposedattentiontransformer_pb_kernel(tc, attn, v, w_proj, b_proj, s
     v_pairs = v.flatten_outer_dims().rearrange("(g p i s) e -> g p i (s e)", p=P, i=2, s=CHUNKS)
     shortcut_pairs = shortcut.flatten_outer_dims().rearrange("(g p i) c -> g p i c", p=P, i=2)
     out_pairs = out.flatten_outer_dims().rearrange("(g p i) c -> g p i c", p=P, i=2)
-    w_halves = w_proj.rearrange("j (u k) -> (j u) k", u=SIDES)
 
     with ExitStack() as ctx:
         keep = ctx.enter_context(tc.tile_pool(name="keep", bufs=1))
         work = ctx.enter_context(tc.tile_pool(name="work", bufs=3))
         psum = ctx.enter_context(tc.psum_pool(name="psum", bufs=1))
 
-        def load_blocks(halves, tiles, into, name):
-            start, stop = 2 * P * tiles[0], 2 * P * (tiles[-1] + 1)
-            blocks = keep.tile([P, 2 * len(tiles), HALF_ROW], BF16, name="%s%d" % (name, tiles[0]))
-            nc.sync.dma_start(out=blocks[:], in_=halves[start:stop, :].rearrange("(i p) x -> p i x", p=P))
-            for n, i in enumerate(tiles):
-                into[i] = blocks[:, 2 * n : 2 * n + 2, :]
+        def load_w(tiles):
+            rows = keep.tile([P, len(tiles), C], BF16, name="w_sb%d" % tiles[0])
+            nc.sync.dma_start(
+                out=rows[:], in_=w_proj[tiles[0] * P : (tiles[-1] + 1) * P, :].rearrange("(n p) k -> p n k", p=P)
+            )
+            for n, j in enumerate(tiles):
+                w_sb[j] = rows[:, n, :]
 
         def load_v(tiles):
             group, start = tiles[0] // 2, tiles[0] % 2
@@ -70,12 +66,12 @@ def tile_transposedattentiontransformer_pb_kernel(tc, attn, v, w_proj, b_proj, s
 
         zeros = keep.tile([P, BANK], BF16, name="zeros")
         nc.vector.memset(zeros[:], 0.0)
+        bias_rows = keep.tile([P, C], BF16, name="bias_rows")
+        nc.vector.memset(bias_rows[:], 0.0)
         ident = keep.tile([P, P], BF16, name="ident")
         make_identity(nc, ident[:])
         ones = keep.tile([P, P], BF16, name="ones")
         nc.vector.memset(ones[:], 1.0)
-        bias_rows = keep.tile([P, C], BF16, name="bias_rows")
-        nc.vector.memset(bias_rows[:], 0.0)
 
         attn_sb, attn_T = {}, {}
         v_sb, w_sb, shortcut_sb = {}, {}, {}
@@ -125,9 +121,7 @@ def tile_transposedattentiontransformer_pb_kernel(tc, attn, v, w_proj, b_proj, s
 
         def copy_y(i):
             grouped_y[i] = work.tile([P, PASSES, P, PACK], BF16, align_bytes=64, name="grouped")
-            chunks = o_banks[i][:].rearrange("p (u c s) r -> p c r s u", u=SIDES, c=PASSES)
-            for c in range(PASSES):
-                nc.scalar.copy(out=grouped_y[i][:, c].rearrange("p r (s u) -> p r s u", u=SIDES), in_=chunks[:, c])
+            nc.scalar.copy(out=grouped_y[i][:], in_=o_banks[i][:].rearrange("p (c t) r -> p c r t", t=PACK))
 
         def quantise_y(i):
             y_codes[i] = keep.tile([P, PASSES, P], U32, name="y_codes%d" % i, align_bytes=64)
@@ -139,20 +133,15 @@ def tile_transposedattentiontransformer_pb_kernel(tc, attn, v, w_proj, b_proj, s
             )
 
         def transpose_w(j_tile):
-            flipped = psum.tile([P, SIDE_CHUNKS, 2, P], BF16, tag="flip", bufs=3, name="flip_w")
-            for i in range(2):
-                for s in range(SIDE_CHUNKS):
-                    nc.tensor.transpose(flipped[:, s, i, :], w_sb[j_tile][:, i, s * P : (s + 1) * P], ident[:])
+            flipped = psum.tile([P, CHUNKS, P], BF16, tag="flip", bufs=3, name="flip_w")
+            for s in range(CHUNKS):
+                nc.tensor.transpose(flipped[:, s, :], w_sb[j_tile][:, s * P : (s + 1) * P], ident[:])
             flipped_w[j_tile] = flipped
 
         def copy_w(j_tile, copy):
             copy(
-                out=w_grouped[:, :, j_tile * P : (j_tile + 1) * P, :].rearrange("p c j t -> p c (j t)").bitcast(F32).rearrange(
-                    "p c (j s) -> p c j s", s=PAIRS
-                ),
-                in_=flipped_w[j_tile][:].rearrange("p s i q -> p (s i q)").bitcast(F32).rearrange(
-                    "p (c s j) -> p c j s", c=PASSES, s=PAIRS
-                ),
+                out=w_grouped[:, :, j_tile * P : (j_tile + 1) * P, :],
+                in_=flipped_w[j_tile][:].rearrange("p (c t) j -> p c j t", t=PACK),
             )
 
         def quantise_w(half, c):
@@ -190,21 +179,18 @@ def tile_transposedattentiontransformer_pb_kernel(tc, attn, v, w_proj, b_proj, s
         def finish(i, half):
             cols = slice(half * BANK, (half + 1) * BANK)
             nc.vector.tensor_tensor(out=residual[i][:, cols], in0=banks[i, half][:], in1=residual[i][:, cols], op=ADD)
-            if i >= ROW_TILES - 2:
-                nc.sync.dma_start(out=out_pairs[i // 2, :, i % 2, cols], in_=residual[i][:, cols])
-            elif half == 1:
-                nc.sync.dma_start(out=out_pairs[i // 2, :, i % 2, :], in_=residual[i][:])
+            nc.sync.dma_start(out=out_pairs[i // 2, :, i % 2, cols], in_=residual[i][:, cols])
 
         attn_sb[0] = load_attn(0)
         load_v((0,))
-        load_v((1,))
-        load_blocks(w_halves, (0, 1), w_sb, "w_sb")
         nc.sync.dma_start(out=bias_rows[0:1, :], in_=b_proj.rearrange("(o c) -> o c", o=1))
-        load_blocks(w_halves, (2, 3), w_sb, "w_sb")
+        load_v((1,))
+        load_w((0, 1))
+        load_w((2, 3))
         shortcut_sb[0] = load_shortcut(0)
         load_v((2, 3))
-        load_blocks(w_halves, (4, 5), w_sb, "w_sb")
-        load_blocks(w_halves, (6, 7), w_sb, "w_sb")
+        load_w((4, 5))
+        load_w((6, 7))
         shortcut_sb[1] = load_shortcut(1)
         attn_sb[1] = load_attn(1)
         load_v((4, 5))
@@ -223,7 +209,7 @@ def tile_transposedattentiontransformer_pb_kernel(tc, attn, v, w_proj, b_proj, s
 
             def weights(j):
                 transpose_w(j)
-                copy_w(j, nc.vector.tensor_copy if j % 4 == 1 else nc.scalar.copy)
+                copy_w(j, nc.scalar.copy if j in (2, 6, 7) else nc.vector.tensor_copy)
 
             def middle(i):
                 multiply(i, 0)
@@ -242,7 +228,7 @@ def tile_transposedattentiontransformer_pb_kernel(tc, attn, v, w_proj, b_proj, s
             early(1)
             spread_bias(0)
             spread_bias(1)
-            for i in range(2, ROW_TILES):
+            for i in range(ROW_TILES):
                 add_bias(i, nc.gpsimd, 2)
             weights(0)
             multiply(0, 0)
@@ -256,7 +242,6 @@ def tile_transposedattentiontransformer_pb_kernel(tc, attn, v, w_proj, b_proj, s
             multiply(1, 1)
             copy_y(1)
             quantise_y(0)
-            add_bias(0, nc.vector)
             quantise_w(0, 0)
             quantise_w(0, 1)
             early(3)
@@ -266,7 +251,6 @@ def tile_transposedattentiontransformer_pb_kernel(tc, attn, v, w_proj, b_proj, s
             weights(5)
             multiply(2, 1)
             copy_y(2)
-            add_bias(1, nc.vector)
             weights(6)
             quantise_y(2)
             next_bank()

@@ -199,9 +199,10 @@ def tile_transposedattentiontransformer_pb_kernel(tc, attn, v, w_proj, b_proj, s
         shortcut_sb[3] = load_shortcut(3)
 
         with tc.manual_schedule():
-            for n in range(3):
-                warm = psum.tile([P, BANK], F32, tag="acc", bufs=3, name="warm")
-                nc.tensor.matmul(warm[:], lhsT=zeros[:, :P], rhs=zeros[:], start=True, stop=True)
+            def warm_up(count):
+                for n in range(count):
+                    warm = psum.tile([P, BANK], F32, tag="acc", bufs=3, name="warm")
+                    nc.tensor.matmul(warm[:], lhsT=zeros[:, :P], rhs=zeros[:], start=True, stop=True)
 
             def early(i):
                 transpose_v(i)
@@ -223,8 +224,11 @@ def tile_transposedattentiontransformer_pb_kernel(tc, attn, v, w_proj, b_proj, s
 
             banks_left = [(0, 0), (1, 0), (0, 1), (1, 1)] + [(i, half) for i in range(2, ROW_TILES) for half in range(HALVES)]
 
+            warm_up(4)
             transpose_attn(0)
+            warm_up(1)
             early(0)
+            warm_up(1)
             early(1)
             spread_bias(0)
             spread_bias(1)

@@ -78,9 +78,9 @@ def tile_transposedattentiontransformer_pb_kernel(tc, attn, v, w_proj, b_proj, s
         flipped_v, flipped_w, v_T, o_banks, grouped_y = {}, {}, {}, {}, {}
         y_codes, y_scales, residual, banks = {}, {}, {}, {}
         bias_all = keep.tile([P, C], BF16, name="bias_all")
-        w_grouped = keep.tile([P, PASSES, C, PACK], BF16, name="w_grouped", align_bytes=64)
-        w_codes = keep.tile([P, PASSES, C], U32, name="w_codes", align_bytes=64)
-        w_scales = keep.tile([P, PASSES, C], U8, name="w_scales", align_bytes=64)
+        w_grouped = keep.tile([P, HALVES, PASSES, BANK, PACK], BF16, name="w_grouped", align_bytes=64)
+        w_codes = keep.tile([P, HALVES, PASSES, BANK], U32, name="w_codes", align_bytes=64)
+        w_scales = keep.tile([P, HALVES, PASSES, BANK], U8, name="w_scales", align_bytes=64)
 
         def spread_bias(half):
             cols = slice(half * BANK, (half + 1) * BANK)
@@ -139,17 +139,17 @@ def tile_transposedattentiontransformer_pb_kernel(tc, attn, v, w_proj, b_proj, s
             flipped_w[j_tile] = flipped
 
         def copy_w(j_tile, copy):
+            half, start = divmod(j_tile * P, BANK)
             copy(
-                out=w_grouped[:, :, j_tile * P : (j_tile + 1) * P, :],
+                out=w_grouped[:, half, :, start : start + P, :],
                 in_=flipped_w[j_tile][:].rearrange("p (c t) j -> p c j t", t=PACK),
             )
 
-        def quantise_w(half, c):
-            cols = slice(half * BANK, (half + 1) * BANK)
+        def quantise_w(half):
             nc.vector.quantize_mx(
-                out=w_codes[:, c, cols].bitcast(FP8X4),
-                scales=w_scales[:, c, cols],
-                in_=w_grouped[:, c, cols, :].rearrange("p j t -> p (j t)"),
+                out=w_codes[:, half].rearrange("p c j -> p (c j)").bitcast(FP8X4),
+                scales=w_scales[:, half].rearrange("p c j -> p (c j)"),
+                in_=w_grouped[:, half].rearrange("p c j t -> p (c j t)"),
             )
 
         def add_bias(i, engine, pieces=1):
@@ -162,15 +162,14 @@ def tile_transposedattentiontransformer_pb_kernel(tc, attn, v, w_proj, b_proj, s
                 )
 
         def project(i, half):
-            cols = slice(half * BANK, (half + 1) * BANK)
             acc = psum.tile([P, BANK], F32, tag="acc", bufs=3, name="acc")
             for c in range(PASSES):
                 nc.tensor.matmul_mx(
                     out=acc[:],
                     lhsT=y_codes[i][:, c, :].bitcast(FP8X4),
                     lhsT_scale=y_scales[i][:, c, :],
-                    rhs=w_codes[:, c, cols].bitcast(FP8X4),
-                    rhs_scale=w_scales[:, c, cols],
+                    rhs=w_codes[:, half, c, :].bitcast(FP8X4),
+                    rhs_scale=w_scales[:, half, c, :],
                     start=(c == 0),
                     stop=(c == PASSES - 1),
                 )
@@ -226,9 +225,7 @@ def tile_transposedattentiontransformer_pb_kernel(tc, attn, v, w_proj, b_proj, s
 
             warm_up(4)
             transpose_attn(0)
-            warm_up(1)
             early(0)
-            warm_up(1)
             early(1)
             spread_bias(0)
             spread_bias(1)
@@ -246,8 +243,7 @@ def tile_transposedattentiontransformer_pb_kernel(tc, attn, v, w_proj, b_proj, s
             multiply(1, 1)
             copy_y(1)
             quantise_y(0)
-            quantise_w(0, 0)
-            quantise_w(0, 1)
+            quantise_w(0)
             early(3)
             quantise_y(1)
             weights(4)
@@ -263,8 +259,7 @@ def tile_transposedattentiontransformer_pb_kernel(tc, attn, v, w_proj, b_proj, s
             next_bank()
             multiply(3, 1)
             copy_y(3)
-            quantise_w(1, 0)
-            quantise_w(1, 1)
+            quantise_w(1)
             quantise_y(3)
             transpose_attn(1)
             for pair in range(4, ROW_TILES, 2):

@@ -152,14 +152,13 @@ def tile_transposedattentiontransformer_pb_kernel(tc, attn, v, w_proj, b_proj, s
                 in_=w_grouped[:, half].rearrange("p c j t -> p (c j t)"),
             )
 
-        def add_bias(i, engine, pieces=1):
-            residual[i] = keep.tile([P, C], F32, name="residual%d" % i)
-            width = C // pieces
-            for n in range(pieces):
-                cols = slice(n * width, (n + 1) * width)
-                engine.tensor_tensor(
-                    out=residual[i][:, cols], in0=shortcut_sb[i // 2][:, i % 2, cols], in1=bias_all[:, cols], op=ADD
-                )
+        def add_bias(i, half, engine):
+            if i not in residual:
+                residual[i] = keep.tile([P, C], F32, name="residual%d" % i)
+            cols = slice(half * BANK, (half + 1) * BANK)
+            engine.tensor_tensor(
+                out=residual[i][:, cols], in0=shortcut_sb[i // 2][:, i % 2, cols], in1=bias_all[:, cols], op=ADD
+            )
 
         def project(i, half):
             acc = psum.tile([P, BANK], F32, tag="acc", bufs=3, name="acc")
@@ -209,7 +208,7 @@ def tile_transposedattentiontransformer_pb_kernel(tc, attn, v, w_proj, b_proj, s
 
             def weights(j):
                 transpose_w(j)
-                copy_w(j, nc.scalar.copy if j in (2, 6, 7) else nc.vector.tensor_copy)
+                copy_w(j, nc.scalar.copy if j % 2 else nc.vector.tensor_copy)
 
             def middle(i):
                 multiply(i, 0)
@@ -221,59 +220,58 @@ def tile_transposedattentiontransformer_pb_kernel(tc, attn, v, w_proj, b_proj, s
                 project(i, half)
                 finish(i, half)
 
-            banks_left = [(0, 0), (1, 0), (0, 1), (1, 1)] + [(i, half) for i in range(2, ROW_TILES) for half in range(HALVES)]
+            banks_left = [(0, 0), (1, 0), (2, 0), (0, 1), (1, 1), (2, 1), (3, 0), (3, 1)]
+            banks_left += [(i, half) for i in range(4, ROW_TILES) for half in range(HALVES)]
+            vector_adds = ((1, 1), (3, 1))
 
             warm_up(4)
             transpose_attn(0)
             early(0)
-            early(1)
             spread_bias(0)
+            early(1)
             spread_bias(1)
-            for i in range(ROW_TILES):
-                add_bias(i, nc.gpsimd, 2)
+            for i, half in banks_left:
+                if (i, half) not in vector_adds:
+                    add_bias(i, half, nc.gpsimd)
             weights(0)
-            multiply(0, 0)
             weights(1)
-            multiply(0, 1)
-            copy_y(0)
+            middle(0)
             weights(2)
-            multiply(1, 0)
             weights(3)
             early(2)
-            multiply(1, 1)
-            copy_y(1)
+            middle(1)
             quantise_y(0)
             quantise_w(0)
+            add_bias(1, 1, nc.vector)
             early(3)
-            quantise_y(1)
-            weights(4)
             multiply(2, 0)
+            weights(4)
             weights(5)
             multiply(2, 1)
             copy_y(2)
-            weights(6)
-            quantise_y(2)
+            quantise_y(1)
             next_bank()
-            multiply(3, 0)
+            add_bias(3, 1, nc.vector)
+            weights(6)
             weights(7)
+            quantise_y(2)
+            multiply(3, 0)
             next_bank()
             multiply(3, 1)
             copy_y(3)
             quantise_w(1)
-            quantise_y(3)
             transpose_attn(1)
-            for pair in range(4, ROW_TILES, 2):
-                early(pair)
-                early(pair + 1)
+            early(4)
+            early(5)
+            next_bank()
+            for i in range(4, ROW_TILES):
+                middle(i)
+                quantise_y(i - 1)
+                if i + 2 < ROW_TILES:
+                    early(i + 2)
                 next_bank()
                 next_bank()
-                middle(pair)
-                next_bank()
-                quantise_y(pair)
-                middle(pair + 1)
-                next_bank()
-                quantise_y(pair + 1)
-                next_bank()
-                next_bank()
+            next_bank()
+            quantise_y(ROW_TILES - 1)
             while banks_left:
                 next_bank()

@@ -36,13 +36,10 @@ def tile_transposedattentiontransformer_pb_kernel(tc, attn, v, w_proj, b_proj, s
         work = ctx.enter_context(tc.tile_pool(name="work", bufs=3))
         psum = ctx.enter_context(tc.psum_pool(name="psum", bufs=1))
 
-        def load_w(tiles):
-            rows = keep.tile([P, len(tiles), C], BF16, name="w_sb%d" % tiles[0])
-            nc.sync.dma_start(
-                out=rows[:], in_=w_proj[tiles[0] * P : (tiles[-1] + 1) * P, :].rearrange("(n p) k -> p n k", p=P)
-            )
-            for n, j in enumerate(tiles):
-                w_sb[j] = rows[:, n, :]
+        def load_w(pair):
+            w_sb[pair] = keep.tile([P, 2, C], BF16, name="w_pair%d" % pair)
+            rows = w_proj[pair * 2 * P : (pair + 1) * 2 * P, :]
+            nc.sync.dma_start(out=w_sb[pair][:], in_=rows.rearrange("(p i) k -> p i k", i=2))
 
         def load_v(tiles):
             group, start = tiles[0] // 2, tiles[0] % 2
@@ -132,17 +129,19 @@ def tile_transposedattentiontransformer_pb_kernel(tc, attn, v, w_proj, b_proj, s
                 in_=grouped_y[i][:].rearrange("p c r t -> p (c r t)"),
             )
 
-        def transpose_w(j_tile):
-            flipped = psum.tile([P, CHUNKS, P], BF16, tag="flip", bufs=3, name="flip_w")
-            for s in range(CHUNKS):
-                nc.tensor.transpose(flipped[:, s, :], w_sb[j_tile][:, s * P : (s + 1) * P], ident[:])
-            flipped_w[j_tile] = flipped
+        def transpose_w(pair, c):
+            flipped = psum.tile([P, 2, PACK, P], BF16, tag="flip", bufs=3, name="flip_w")
+            for i in range(2):
+                for t in range(PACK):
+                    k = (c * PACK + t) * P
+                    nc.tensor.transpose(flipped[:, i, t, :], w_sb[pair][:, i, k : k + P], ident[:])
+            flipped_w[pair, c] = flipped
 
-        def copy_w(j_tile, copy):
-            half, start = divmod(j_tile * P, BANK)
+        def copy_w(pair, c, copy):
+            half, start = divmod(pair * 2 * P, BANK)
             copy(
-                out=w_grouped[:, half, :, start : start + P, :],
-                in_=flipped_w[j_tile][:].rearrange("p (c t) j -> p c j t", t=PACK),
+                out=w_grouped[:, half, c, start : start + 2 * P, :].rearrange("d (p i) t -> d p i t", i=2),
+                in_=flipped_w[pair, c][:].rearrange("d i t p -> d p i t"),
             )
 
         def quantise_w(half):
@@ -183,12 +182,12 @@ def tile_transposedattentiontransformer_pb_kernel(tc, attn, v, w_proj, b_proj, s
         load_v((0,))
         nc.sync.dma_start(out=bias_rows[0:1, :], in_=b_proj.rearrange("(o c) -> o c", o=1))
         load_v((1,))
-        load_w((0, 1))
-        load_w((2, 3))
+        load_w(0)
+        load_w(1)
         shortcut_sb[0] = load_shortcut(0)
         load_v((2, 3))
-        load_w((4, 5))
-        load_w((6, 7))
+        load_w(2)
+        load_w(3)
         shortcut_sb[1] = load_shortcut(1)
         attn_sb[1] = load_attn(1)
         load_v((4, 5))
@@ -206,9 +205,10 @@ def tile_transposedattentiontransformer_pb_kernel(tc, attn, v, w_proj, b_proj, s
                 transpose_v(i)
                 copy_v(i)
 
-            def weights(j):
-                transpose_w(j)
-                copy_w(j, nc.scalar.copy if j % 2 else nc.vector.tensor_copy)
+            def weights(pair):
+                for c, copy in enumerate((nc.vector.tensor_copy, nc.scalar.copy)):
+                    transpose_w(pair, c)
+                    copy_w(pair, c, copy)
 
             def middle(i):
                 multiply(i, 0)
@@ -234,10 +234,8 @@ def tile_transposedattentiontransformer_pb_kernel(tc, attn, v, w_proj, b_proj, s
                 if (i, half) not in vector_adds:
                     add_bias(i, half, nc.gpsimd)
             weights(0)
-            weights(1)
             middle(0)
-            weights(2)
-            weights(3)
+            weights(1)
             early(2)
             middle(1)
             quantise_y(0)
@@ -245,15 +243,13 @@ def tile_transposedattentiontransformer_pb_kernel(tc, attn, v, w_proj, b_proj, s
             add_bias(1, 1, nc.vector)
             early(3)
             multiply(2, 0)
-            weights(4)
-            weights(5)
+            weights(2)
             multiply(2, 1)
             copy_y(2)
             quantise_y(1)
             next_bank()
             add_bias(3, 1, nc.vector)
-            weights(6)
-            weights(7)
+            weights(3)
             quantise_y(2)
             multiply(3, 0)
             next_bank()

@@ -206,9 +206,9 @@ def tile_transposedattentiontransformer_pb_kernel(tc, attn, v, w_proj, b_proj, s
                 copy_v(i)
 
             def weights(pair):
-                for c, copy in enumerate((nc.vector.tensor_copy, nc.scalar.copy)):
+                for c in range(PASSES):
                     transpose_w(pair, c)
-                    copy_w(pair, c, copy)
+                    copy_w(pair, c, nc.scalar.copy if c == 1 and pair != 1 else nc.vector.tensor_copy)
 
             def middle(i):
                 multiply(i, 0)
@@ -227,8 +227,8 @@ def tile_transposedattentiontransformer_pb_kernel(tc, attn, v, w_proj, b_proj, s
             warm_up(4)
             transpose_attn(0)
             early(0)
-            spread_bias(0)
             early(1)
+            spread_bias(0)
             spread_bias(1)
             for i, half in banks_left:
                 if (i, half) not in vector_adds:
@@ -236,24 +236,22 @@ def tile_transposedattentiontransformer_pb_kernel(tc, attn, v, w_proj, b_proj, s
             weights(0)
             middle(0)
             weights(1)
-            early(2)
             middle(1)
             quantise_y(0)
             quantise_w(0)
             add_bias(1, 1, nc.vector)
+            early(2)
             early(3)
-            multiply(2, 0)
             weights(2)
-            multiply(2, 1)
-            copy_y(2)
+            middle(2)
             quantise_y(1)
             next_bank()
             add_bias(3, 1, nc.vector)
             weights(3)
             quantise_y(2)
             multiply(3, 0)
-            next_bank()
             multiply(3, 1)
+            next_bank()
             copy_y(3)
             quantise_w(1)
             transpose_attn(1)
@@ -263,11 +261,11 @@ def tile_transposedattentiontransformer_pb_kernel(tc, attn, v, w_proj, b_proj, s
             for i in range(4, ROW_TILES):
                 middle(i)
                 quantise_y(i - 1)
-                if i + 2 < ROW_TILES:
-                    early(i + 2)
                 next_bank()
                 next_bank()
-            next_bank()
+                if i == 4:
+                    early(6)
+                    early(7)
             quantise_y(ROW_TILES - 1)
             while banks_left:
                 next_bank()

@@ -208,7 +208,7 @@ def tile_transposedattentiontransformer_pb_kernel(tc, attn, v, w_proj, b_proj, s
             def weights(pair):
                 for c in range(PASSES):
                     transpose_w(pair, c)
-                    copy_w(pair, c, nc.scalar.copy if c == 1 and pair != 1 else nc.vector.tensor_copy)
+                    copy_w(pair, c, nc.scalar.copy if pair == 2 or (c == 1 and pair != 1) else nc.vector.tensor_copy)
 
             def middle(i):
                 multiply(i, 0)
@@ -222,7 +222,7 @@ def tile_transposedattentiontransformer_pb_kernel(tc, attn, v, w_proj, b_proj, s
 
             banks_left = [(0, 0), (1, 0), (2, 0), (0, 1), (1, 1), (2, 1), (3, 0), (3, 1)]
             banks_left += [(i, half) for i in range(4, ROW_TILES) for half in range(HALVES)]
-            vector_adds = ((1, 1), (3, 1))
+            vector_adds = ((1, 1), (3, 1), (5, 1))
 
             warm_up(4)
             transpose_attn(0)
@@ -261,6 +261,8 @@ def tile_transposedattentiontransformer_pb_kernel(tc, attn, v, w_proj, b_proj, s
             for i in range(4, ROW_TILES):
                 middle(i)
                 quantise_y(i - 1)
+                if (i, 1) in vector_adds:
+                    add_bias(i, 1, nc.vector)
                 next_bank()
                 next_bank()
                 if i == 4:

@@ -252,22 +252,21 @@ def tile_transposedattentiontransformer_pb_kernel(tc, attn, v, w_proj, b_proj, s
             multiply(3, 0)
             multiply(3, 1)
             next_bank()
-            copy_y(3)
             quantise_w(1)
             transpose_attn(1)
             early(4)
             early(5)
+            copy_y(3)
             next_bank()
             for i in range(4, ROW_TILES):
                 middle(i)
                 quantise_y(i - 1)
-                if (i, 1) in vector_adds:
-                    add_bias(i, 1, nc.vector)
                 next_bank()
                 next_bank()
                 if i == 4:
                     early(6)
                     early(7)
+                    add_bias(5, 1, nc.vector)
             quantise_y(ROW_TILES - 1)
             while banks_left:
                 next_bank()

from contextlib import ExitStack

import concourse.mybir as mybir
from concourse.masks import make_identity

BF16 = mybir.dt.bfloat16
F32 = mybir.dt.float32
U32 = mybir.dt.uint32
U8 = mybir.dt.uint8
FP8X4 = mybir.dt.float8_e4m3fn_x4
ADD = mybir.AluOpType.add

P = 128
BATCH, HEADS, TOKENS, C = 2, 8, 512, 1024
CHUNKS = C // P
PACK = 4
PASSES = C // (P * PACK)
ROW_TILES = BATCH * TOKENS // P
HEAD_ROWS = TOKENS // CHUNKS
GROUPS = ROW_TILES // 2
BANK = 512
HALVES = C // BANK
ATTN_ROWS = HEADS * P // P

FLOPS = 2 * BATCH * HEADS * P * P * TOKENS + 2 * BATCH * TOKENS * C * C


def tile_transposedattentiontransformer_pb_kernel(tc, attn, v, w_proj, b_proj, shortcut, out):
    nc = tc.nc
    v_pairs = v.flatten_outer_dims().rearrange("(g p i s) e -> g p i (s e)", p=P, i=2, s=CHUNKS)
    shortcut_pairs = shortcut.flatten_outer_dims().rearrange("(g p i) c -> g p i c", p=P, i=2)
    out_pairs = out.flatten_outer_dims().rearrange("(g p i) c -> g p i c", p=P, i=2)

    with ExitStack() as ctx:
        keep = ctx.enter_context(tc.tile_pool(name="keep", bufs=1))
        work = ctx.enter_context(tc.tile_pool(name="work", bufs=3))
        psum = ctx.enter_context(tc.psum_pool(name="psum", bufs=1))

        def load_w(pair):
            w_sb[pair] = keep.tile([P, 2, C], BF16, name="w_pair%d" % pair)
            rows = w_proj[pair * 2 * P : (pair + 1) * 2 * P, :]
            nc.sync.dma_start(out=w_sb[pair][:], in_=rows.rearrange("(p i) k -> p i k", i=2))

        def load_v(tiles):
            group, start = tiles[0] // 2, tiles[0] % 2
            rows = keep.tile([P, len(tiles), C], BF16, name="v_sb%d" % tiles[0])
            nc.sync.dma_start(out=rows[:], in_=v_pairs[group, :, start : start + len(tiles), :])
            for n, i in enumerate(tiles):
                v_sb[i] = rows[:, n, :]

        def load_shortcut(group):
            pair = keep.tile([P, 2, C], BF16, name="shortcut_sb%d" % group)
            nc.sync.dma_start(out=pair[:], in_=shortcut_pairs[group])
            return pair

        def load_attn(b):
            rows = keep.tile([P, ATTN_ROWS, P], BF16, name="attn_sb%d" % b)
            nc.sync.dma_start(out=rows[:], in_=attn[b].rearrange("g (q i) e -> (g q) i e", i=ATTN_ROWS))
            return rows

        def words(ap, merge):
            return ap.rearrange(merge).bitcast(F32)

        zeros = keep.tile([P, BANK], BF16, name="zeros")
        nc.vector.memset(zeros[:], 0.0)
        bias_rows = keep.tile([P, C], BF16, name="bias_rows")
        nc.vector.memset(bias_rows[:], 0.0)
        ident = keep.tile([P, P], BF16, name="ident")
        make_identity(nc, ident[:])
        ones = keep.tile([P, P], BF16, name="ones")
        nc.vector.memset(ones[:], 1.0)

        attn_sb, attn_T = {}, {}
        v_sb, w_sb, shortcut_sb = {}, {}, {}
        flipped_v, flipped_w, v_T, o_banks, grouped_y = {}, {}, {}, {}, {}
        y_codes, y_scales, residual, banks = {}, {}, {}, {}
        bias_all = keep.tile([P, C], BF16, name="bias_all")
        w_grouped = keep.tile([P, HALVES, PASSES, BANK, PACK], BF16, name="w_grouped", align_bytes=64)
        w_codes = keep.tile([P, HALVES, PASSES, BANK], U32, name="w_codes", align_bytes=64)
        w_scales = keep.tile([P, HALVES, PASSES, BANK], U8, name="w_scales", align_bytes=64)

        def spread_bias(half):
            cols = slice(half * BANK, (half + 1) * BANK)
            spread = psum.tile([P, BANK], F32, tag="acc", bufs=3, name="spread")
            nc.tensor.matmul(spread[:], lhsT=ones[:], rhs=bias_rows[:, cols], start=True, stop=True)
            nc.scalar.copy(out=bias_all[:, cols], in_=spread[:])

        def transpose_attn(b):
            flipped = psum.tile([P, ATTN_ROWS, P], BF16, tag="flip", bufs=3, name="flip_a")
            for i in range(ATTN_ROWS):
                nc.tensor.transpose(flipped[:, i, :], attn_sb[b][:, i, :], ident[:])
            attn_T[b] = keep.tile([P, HEADS, P], BF16, name="attn_T%d" % b)
            for copy, heads in ((nc.scalar.copy, slice(0, HEADS // 2)), (nc.vector.tensor_copy, slice(HEADS // 2, HEADS))):
                copy(
                    out=attn_T[b][:, heads, :].rearrange("p g (q i) -> p (g q) i", i=ATTN_ROWS),
                    in_=flipped[:].rearrange("p i (g q) -> p g q i", g=HEADS)[:, heads].rearrange("p g q i -> p (g q) i"),
                )

        def transpose_v(i):
            flipped = psum.tile([P, CHUNKS, P], BF16, tag="flip", bufs=3, name="flip_v")
            for s in range(CHUNKS):
                nc.tensor.transpose(flipped[:, s, :], v_sb[i][:, s * P : (s + 1) * P], ident[:])
            flipped_v[i] = flipped

        def copy_v(i):
            v_T[i] = work.tile([P, CHUNKS, P], BF16, name="v_T")
            nc.scalar.copy(out=words(v_T[i][:], "p s r -> p (s r)"), in_=words(flipped_v[i][:], "p s r -> p (s r)"))

        def multiply(i, part):
            if part == 0:
                o_banks[i] = psum.tile([P, CHUNKS, P], BF16, tag="o", bufs=2, name="o")
            for n in (2 * part, 2 * part + 1):
                head = 4 * (i // 2) + n
                rows = slice(n * P // 4, (n + 1) * P // 4)
                nc.tensor.matmul(
                    o_banks[i][:, :, rows], lhsT=attn_T[head // HEADS][:, head % HEADS, :], rhs=v_T[i][:, :, rows], start=True, stop=True
                )

        def copy_y(i):
            grouped_y[i] = work.tile([P, PASSES, P, PACK], BF16, align_bytes=64, name="grouped")
            nc.scalar.copy(out=grouped_y[i][:], in_=o_banks[i][:].rearrange("p (c t) r -> p c r t", t=PACK))

        def quantise_y(i):
            y_codes[i] = keep.tile([P, PASSES, P], U32, name="y_codes%d" % i, align_bytes=64)
            y_scales[i] = keep.tile([P, PASSES, P], U8, name="y_scales%d" % i, align_bytes=64)
            nc.vector.quantize_mx(
                out=y_codes[i][:].rearrange("p c r -> p (c r)").bitcast(FP8X4),
                scales=y_scales[i][:].rearrange("p c r -> p (c r)"),
                in_=grouped_y[i][:].rearrange("p c r t -> p (c r t)"),
            )

        def transpose_w(pair, c):
            flipped = psum.tile([P, 2, PACK, P], BF16, tag="flip", bufs=3, name="flip_w")
            for i in range(2):
                for t in range(PACK):
                    k = (c * PACK + t) * P
                    nc.tensor.transpose(flipped[:, i, t, :], w_sb[pair][:, i, k : k + P], ident[:])
            flipped_w[pair, c] = flipped

        def copy_w(pair, c, copy):
            half, start = divmod(pair * 2 * P, BANK)
            copy(
                out=w_grouped[:, half, c, start : start + 2 * P, :].rearrange("d (p i) t -> d p i t", i=2),
                in_=flipped_w[pair, c][:].rearrange("d i t p -> d p i t"),
            )

        def quantise_w(half):
            nc.vector.quantize_mx(
                out=w_codes[:, half].rearrange("p c j -> p (c j)").bitcast(FP8X4),
                scales=w_scales[:, half].rearrange("p c j -> p (c j)"),
                in_=w_grouped[:, half].rearrange("p c j t -> p (c j t)"),
            )

        def add_bias(i, half, engine):
            if i not in residual:
                residual[i] = keep.tile([P, C], F32, name="residual%d" % i)
            cols = slice(half * BANK, (half + 1) * BANK)
            engine.tensor_tensor(
                out=residual[i][:, cols], in0=shortcut_sb[i // 2][:, i % 2, cols], in1=bias_all[:, cols], op=ADD
            )

        def project(i, half):
            acc = psum.tile([P, BANK], F32, tag="acc", bufs=3, name="acc")
            for c in range(PASSES):
                nc.tensor.matmul_mx(
                    out=acc[:],
                    lhsT=y_codes[i][:, c, :].bitcast(FP8X4),
                    lhsT_scale=y_scales[i][:, c, :],
                    rhs=w_codes[:, half, c, :].bitcast(FP8X4),
                    rhs_scale=w_scales[:, half, c, :],
                    start=(c == 0),
                    stop=(c == PASSES - 1),
                )
            banks[i, half] = acc

        def finish(i, half):
            cols = slice(half * BANK, (half + 1) * BANK)
            nc.vector.tensor_tensor(out=residual[i][:, cols], in0=banks[i, half][:], in1=residual[i][:, cols], op=ADD)
            nc.sync.dma_start(out=out_pairs[i // 2, :, i % 2, cols], in_=residual[i][:, cols])

        attn_sb[0] = load_attn(0)
        load_v((0,))
        nc.sync.dma_start(out=bias_rows[0:1, :], in_=b_proj.rearrange("(o c) -> o c", o=1))
        load_v((1,))
        load_w(0)
        load_w(1)
        shortcut_sb[0] = load_shortcut(0)
        load_v((2, 3))
        load_w(2)
        load_w(3)
        shortcut_sb[1] = load_shortcut(1)
        attn_sb[1] = load_attn(1)
        load_v((4, 5))
        load_v((6, 7))
        shortcut_sb[2] = load_shortcut(2)
        shortcut_sb[3] = load_shortcut(3)

        with tc.manual_schedule():
            def warm_up(count):
                for n in range(count):
                    warm = psum.tile([P, BANK], F32, tag="acc", bufs=3, name="warm")
                    nc.tensor.matmul(warm[:], lhsT=zeros[:, :P], rhs=zeros[:], start=True, stop=True)

            def early(i):
                transpose_v(i)
                copy_v(i)

            def weights(pair):
                for c in range(PASSES):
                    transpose_w(pair, c)
                    copy_w(pair, c, nc.scalar.copy if pair == 2 or (c == 1 and pair != 1) else nc.vector.tensor_copy)

            def middle(i):
                multiply(i, 0)
                multiply(i, 1)
                copy_y(i)

            def next_bank():
                i, half = banks_left.pop(0)
                project(i, half)
                finish(i, half)

            banks_left = [(0, 0), (1, 0), (2, 0), (0, 1), (1, 1), (2, 1), (3, 0), (3, 1)]
            banks_left += [(i, half) for i in range(4, ROW_TILES) for half in range(HALVES)]
            vector_adds = ((1, 1), (3, 1), (5, 1))

            warm_up(4)
            transpose_attn(0)
            early(0)
            early(1)
            spread_bias(0)
            spread_bias(1)
            for i, half in banks_left:
                if (i, half) not in vector_adds:
                    add_bias(i, half, nc.gpsimd)
            weights(0)
            middle(0)
            weights(1)
            middle(1)
            quantise_y(0)
            quantise_w(0)
            add_bias(1, 1, nc.vector)
            early(2)
            early(3)
            weights(2)
            middle(2)
            quantise_y(1)
            next_bank()
            add_bias(3, 1, nc.vector)
            weights(3)
            quantise_y(2)
            multiply(3, 0)
            multiply(3, 1)
            next_bank()
            quantise_w(1)
            transpose_attn(1)
            early(4)
            early(5)
            copy_y(3)
            next_bank()
            for i in range(4, ROW_TILES):
                middle(i)
                quantise_y(i - 1)
                next_bank()
                next_bank()
                if i == 4:
                    early(6)
                    early(7)
                    add_bias(5, 1, nc.vector)
            quantise_y(ROW_TILES - 1)
            while banks_left:
                next_bank()
